import numpy as np
import ml_dtypes


def mxq(x, axis, fmt="e4m3"):
    dtype, down = {"e4m3": (ml_dtypes.float8_e4m3fn, 7), "e5m2": (ml_dtypes.float8_e5m2, 14)}[fmt]
    v = np.moveaxis(np.asarray(x, np.float32).astype(ml_dtypes.bfloat16).astype(np.float64), axis, -1)
    blocks = v.reshape(v.shape[:-1] + (-1, 32))
    amax = np.abs(blocks).max(-1, keepdims=True)
    byte = np.maximum(np.where(amax > 0, np.frexp(amax)[1] - 1 + 127, 0) - down, 1)
    scale = np.exp2(byte - 127.0)
    codes = (blocks / scale).astype(np.float32).astype(dtype).astype(np.float64)
    return np.moveaxis((codes * scale).reshape(v.shape), -1, axis)


WIDE = False


def mx_kscale(k):
    if not WIDE:
        return np.ones(k)
    levels = np.array([10, -10, 5, -5, 0])
    a = np.random.permutation(np.resize(levels, k // 512 * 4)).reshape(k // 512, 4)
    idx = np.arange(k)
    return np.exp2(a[idx // 512, idx % 128 // 32])


BF16 = ml_dtypes.bfloat16


def bf(x):
    return np.asarray(x, np.float32).astype(BF16)


def f64(x):
    return np.asarray(x).astype(np.float64)


B, CI, R, CO, H, W, D, K, PAD = 2, 512, 1024, 1024, 8, 8, 16, 3, 1
N = H * W * D


def setup_inputs():
    s, u = mx_kscale(CI), mx_kscale(R)
    return {"x": bf(np.random.standard_normal((B, CI, H, W, D)) * s[None, :, None, None, None]),
            "U_k_h": bf(np.random.standard_normal((K, R)) / np.sqrt(K)),
            "U_k_w": bf(np.random.standard_normal((K, R)) / np.sqrt(K)),
            "U_k_d": bf(np.random.standard_normal((K, R)) / np.sqrt(K)),
            "U_c_in": bf(np.random.standard_normal((CI, R)) / np.sqrt(CI) / s[:, None] * u[None, :]),
            "U_c_out": bf(np.random.standard_normal((R, CO)) / np.sqrt(R) / u[:, None]),
            "bias": bf(np.random.standard_normal(CO) * 0.5)}


def reference(x, U_k_h, U_k_w, U_k_d, U_c_in, U_c_out, bias):
    kh, kw, kd = f64(U_k_h), f64(U_k_w), f64(U_k_d)
    t = (mxq(f64(U_c_in), 0, "e4m3").T @ mxq(f64(x).reshape(B, CI, N), 1, "e4m3")).reshape(B, R, H, W, D)
    t = np.pad(t, ((0, 0), (0, 0), (PAD, PAD), (PAD, PAD), (PAD, PAD)))
    t = sum(t[:, :, k:k + H, :, :] * kh[k][None, :, None, None, None] for k in range(K))
    t = sum(t[:, :, :, k:k + W, :] * kw[k][None, :, None, None, None] for k in range(K))
    t = sum(t[:, :, :, :, k:k + D] * kd[k][None, :, None, None, None] for k in range(K))
    out = (mxq(f64(U_c_out), 0, "e4m3").T @ mxq(t.reshape(B, R, N), 1, "e4m3")).reshape(B, CO, H, W, D)
    return out + f64(bias)[None, :, None, None, None]

@@ -1,0 +1,327 @@
+from contextlib import ExitStack
+
+import concourse.mybir as mybir
+from concourse.masks import make_identity
+
+F32 = mybir.dt.float32
+BF16 = mybir.dt.bfloat16
+U32 = mybir.dt.uint32
+U8 = mybir.dt.uint8
+FP8X4 = mybir.dt.float8_e4m3fn_x4
+MULT = mybir.AluOpType.mult
+ADD = mybir.AluOpType.add
+COPY = mybir.ActivationFunctionType.Copy
+IDENT = mybir.ActivationFunctionType.Identity
+
+P = 128
+B, CI, R, CO, H, W, D = 2, 512, 1024, 1024, 8, 8, 16
+N = H * W * D
+HALF = 512
+NU = 32
+PE_TILES = (1, 4, 6)
+FLOPS = 2 * B * N * (CI * R + R * CO) + 2 * 9 * B * R * N
+
+
+def regroup(copy, dst, src):
+    copy(
+        out=dst.rearrange("p (c i) t -> p c t i", i=4),
+        in_=src.rearrange("p t (c i) -> p c t i", i=4),
+    )
+
+
+def rows(ap, r0, r1):
+    return ap.rearrange("p (h c) -> p h c", h=4)[:, r0:r1, :]
+
+
+def tile_lowrankconv3d_pa_kernel(tc, x, U_k_h, U_k_w, U_k_d, U_c_in, U_c_out, bias, out):
+    nc = tc.nc
+    with ExitStack() as ctx:
+        keep = ctx.enter_context(tc.tile_pool(name="keep", bufs=1))
+        grp_pool = ctx.enter_context(tc.tile_pool(name="grp", bufs=4))
+        t1_pool = ctx.enter_context(tc.tile_pool(name="t1p", bufs=6))
+        t2_pool = ctx.enter_context(tc.tile_pool(name="t2p", bufs=6))
+        t3_pool = ctx.enter_context(tc.tile_pool(name="t3p", bufs=3))
+        o_pool = ctx.enter_context(tc.tile_pool(name="op", bufs=8))
+        ps = ctx.enter_context(tc.psum_pool(name="ps", bufs=8))
+        ctx.enter_context(tc.manual_schedule())
+
+        x_raw = keep.tile([P, B, 4, N], BF16, name="x_raw")
+        ui_raw = keep.tile([P, 4, R], BF16, name="ui_raw")
+        uo_raw = keep.tile([P, 2, 4, CO], BF16, name="uo_raw")
+        x_codes = keep.tile([P, B, N], U32, name="x_codes", align_bytes=64)
+        x_scales = keep.tile([P, B, N], U8, name="x_scales", align_bytes=64)
+        ui_codes = keep.tile([P, R], U32, name="ui_codes", align_bytes=64)
+        ui_scales = keep.tile([P, R], U8, name="ui_scales", align_bytes=64)
+        uo_codes = keep.tile([P, 2, CO], U32, name="uo_codes", align_bytes=64)
+        uo_scales = keep.tile([P, 2, CO], U8, name="uo_scales", align_bytes=64)
+        t3_codes = keep.tile([P, 4, 2, HALF], U32, name="t3_codes", align_bytes=64)
+        t3_scales = keep.tile([P, 4, 2, HALF], U8, name="t3_scales", align_bytes=64)
+        tap_bf = keep.tile([P, 3, 8, 4], BF16, name="tap_bf")
+        tapf = keep.tile([P, 3, 8, 4], F32, name="tapf")
+        bias_bf = keep.tile([P, 8], BF16, name="bias_bf")
+        biasf = keep.tile([P, 8], F32, name="biasf")
+        pads = [keep.tile([P, 4, 160], F32, name="t1pad%d" % k) for k in range(len(PE_TILES))]
+        if PE_TILES:
+            ident = keep.tile([P, P], F32, name="ident")
+            diag = keep.tile([P, 3 * len(PE_TILES), P], F32, name="diag")
+            make_identity(nc, ident[:])
+            for t in pads:
+                nc.gpsimd.memset(t[:], 0.0)
+
+        xv = [x[b].rearrange("(p t) h w d -> p t (h w d)", t=4) for b in range(B)]
+        uiv = U_c_in.rearrange("(p t) r -> p t r", t=4)
+        uov = U_c_out.rearrange("(g p t) c -> g p t c", g=2, t=4)
+        nc.sync.dma_start(out=ui_raw[:, :, 0:HALF], in_=uiv[:, :, 0:HALF])
+        nc.sync.dma_start(out=x_raw[:, 0, :, 0:HALF], in_=xv[0][:, :, 0:HALF])
+        nc.sync.dma_start(out=x_raw[:, 0, :, HALF:N], in_=xv[0][:, :, HALF:N])
+        nc.sync.dma_start(out=ui_raw[:, :, HALF:R], in_=uiv[:, :, HALF:R])
+        with nc.allow_non_contiguous_dma(reason="taps come in 8-byte runs"):
+            for f, u in enumerate((U_k_h, U_k_w, U_k_d)):
+                nc.sync.dma_start(
+                    out=tap_bf[:, f, 0:6, :],
+                    in_=u.rearrange("k r -> (k r)").rearrange("(q m j) -> m q j", q=6, m=P, j=4),
+                )
+        nc.sync.dma_start(out=uo_raw[:, 0, :, :], in_=uov[0])
+        nc.sync.dma_start(out=uo_raw[:, 1, :, :], in_=uov[1])
+        nc.sync.dma_start(out=x_raw[:, 1, :, :], in_=xv[1])
+        with nc.allow_non_contiguous_dma(reason="bias: one element a partition"):
+            nc.sync.dma_start(out=bias_bf[:], in_=bias.rearrange("(i m) -> m i", i=8, m=P))
+
+        vcopy = nc.vector.tensor_copy
+        scopy = nc.scalar.copy
+
+        def tap(f, k, tl):
+            return tapf[:, f, k * 2 + tl // 4, tl % 4 : tl % 4 + 1]
+
+        def quant(src, codes, scales):
+            nc.vector.quantize_mx(out=codes.bitcast(FP8X4), scales=scales, in_=src.rearrange("p w t -> p (w t)"))
+
+        def new_grp():
+            return grp_pool.tile([P, HALF, 4], BF16, name="grp", align_bytes=64)
+
+        def stt(o, a, s, c):
+            nc.vector.scalar_tensor_tensor(out=o, in0=a, scalar=s, in1=c, op0=MULT, op1=ADD)
+
+        def ui_regroup(copy, grp, g, j0, j1):
+            copy(
+                out=grp[:, j0 * P : j1 * P, :].rearrange("p (j m) t -> p j m t", j=j1 - j0),
+                in_=ui_raw[:, :, g * HALF : (g + 1) * HALF].rearrange("p t (m j) -> p j m t", j=4)[:, j0:j1],
+            )
+
+        g_ui0 = new_grp()
+        g_x00 = new_grp()
+        g_x01 = new_grp()
+        g_ui1 = new_grp()
+        ui_regroup(vcopy, g_ui0, 0, 0, 1)
+        ui_regroup(scopy, g_ui0, 0, 1, 4)
+        regroup(vcopy, g_x00[:], x_raw[:, 0, :, 0:HALF])
+        quant(g_ui0[:, 0:P, :], ui_codes[:, 0:P], ui_scales[:, 0:P])
+        quant(g_x00[:], x_codes[:, 0, 0:HALF], x_scales[:, 0, 0:HALF])
+        regroup(vcopy, g_x01[:], x_raw[:, 0, :, HALF:N])
+        quant(g_ui0[:, P : 2 * P, :], ui_codes[:, P : 2 * P], ui_scales[:, P : 2 * P])
+        quant(g_x01[:], x_codes[:, 0, HALF:N], x_scales[:, 0, HALF:N])
+        quant(g_ui0[:, 2 * P : 4 * P, :], ui_codes[:, 2 * P : 4 * P], ui_scales[:, 2 * P : 4 * P])
+        ui_regroup(scopy, g_ui1, 1, 0, 4)
+        nc.scalar.copy(out=tapf[:, :, 0:6, :], in_=tap_bf[:, :, 0:6, :])
+        for n_, tl in enumerate(PE_TILES):
+            for k in range(3):
+                nc.gpsimd.tensor_scalar(
+                    out=diag[:, 3 * n_ + k, :], in0=ident[:], scalar1=tap(1, k, tl), scalar2=0.0, op0=MULT, op1=ADD
+                )
+
+        t0a, t0b, t1s, t2s, t3s = {}, {}, {}, {}, {}
+
+        def valid(q):
+            return 0 <= q < NU
+
+        def on_pe(q):
+            return (q % 8) in PE_TILES
+
+        def mx(o, lc, ls, rc, rs, start, stop):
+            nc.tensor.matmul_mx(
+                out=o, lhsT=lc.bitcast(FP8X4), lhsT_scale=ls, rhs=rc.bitcast(FP8X4), rhs_scale=rs, start=start, stop=stop
+            )
+
+        def pe_t0(q):
+            c, tl = q // 8, q % 8
+            b, hh = c // 2, c % 2
+            mc = slice(tl * P, (tl + 1) * P)
+            t0a[q] = ps.tile([P, HALF], F32, name="bank")
+            t0b[q] = ps.tile([P, HALF], F32, name="bank")
+            for t, lo in ((t0a[q], hh * HALF), (t0b[q], 128 + hh * 256)):
+                mx(t[:], ui_codes[:, mc], ui_scales[:, mc], x_codes[:, b, lo : lo + HALF], x_scales[:, b, lo : lo + HALF], True, True)
+
+        def t1rows(q, r0, r1):
+            if on_pe(q):
+                return t1s[q][:, r0:r1, 16:144]
+            return rows(t1s[q][:], r0, r1)
+
+        def s_hc(q):
+            if on_pe(q):
+                t1s[q] = pads[PE_TILES.index(q % 8)]
+            else:
+                t1s[q] = t1_pool.tile([P, HALF], F32, name="t1")
+            nc.scalar.activation(out=t1rows(q, 0, 4), in_=rows(t0a[q][:], 0, 4), func=COPY, scale=tap(0, 1, q % 8))
+
+        def v_h(q):
+            tl, hh = q % 8, (q // 8) % 2
+            if hh == 0:
+                return [
+                    lambda: stt(t1rows(q, 1, 4), rows(t0a[q][:], 0, 3), tap(0, 0, tl), t1rows(q, 1, 4)),
+                    lambda: stt(t1rows(q, 0, 4), rows(t0b[q][:], 0, 4), tap(0, 2, tl), t1rows(q, 0, 4)),
+                ]
+            return [
+                lambda: stt(t1rows(q, 0, 4), rows(t0b[q][:], 0, 4), tap(0, 0, tl), t1rows(q, 0, 4)),
+                lambda: stt(t1rows(q, 0, 3), rows(t0a[q][:], 1, 4), tap(0, 2, tl), t1rows(q, 0, 3)),
+            ]
+
+        def s_wc(q):
+            t2s[q] = t2_pool.tile([P, HALF], F32, name="t2")
+            nc.scalar.activation(out=t2s[q][:], in_=t1s[q][:], func=COPY, scale=tap(1, 1, q % 8))
+
+        def pe_w(q):
+            t2s[q] = ps.tile([P, HALF], F32, name="bank")
+            n_ = PE_TILES.index(q % 8)
+            for k in range(3):
+                nc.tensor.matmul(
+                    out=rows(t2s[q][:], 0, 4),
+                    lhsT=diag[:, 3 * n_ + k, :],
+                    rhs=t1s[q][:, :, 16 * k : 16 * k + 128],
+                    start=(k == 0),
+                    stop=(k == 2),
+                )
+
+        def v_w(q):
+            tl = q % 8
+            a, o = rows(t1s[q][:], 0, 4), rows(t2s[q][:], 0, 4)
+            return [
+                lambda: stt(o[:, :, 16:128], a[:, :, 0:112], tap(1, 0, tl), o[:, :, 16:128]),
+                lambda: stt(o[:, :, 0:112], a[:, :, 16:128], tap(1, 2, tl), o[:, :, 0:112]),
+            ]
+
+        def s_dc(q):
+            key = q // 4
+            if q % 4 == 0:
+                t3s[key] = t3_pool.tile([P, 4, HALF], F32, name="t3f")
+            nc.scalar.activation(out=t3s[key][:, q % 4, :], in_=t2s[q][:], func=COPY, scale=tap(2, 1, q % 8))
+
+        def v_d(q):
+            tl = q % 8
+            a = t2s[q][:].rearrange("p (r d) -> p r d", d=D)
+            o = t3s[q // 4][:, q % 4, :].rearrange("p (r d) -> p r d", d=D)
+            return [
+                lambda: stt(o[:, :, 1:16], a[:, :, 0:15], tap(2, 0, tl), o[:, :, 1:16]),
+                lambda: stt(o[:, :, 0:15], a[:, :, 1:16], tap(2, 2, tl), o[:, :, 0:15]),
+            ]
+
+        jobs = {}
+        grps, accs = {}, {}
+
+        def at(kind, step, fn):
+            jobs[(kind, step)] = jobs.get((kind, step), []) + [fn]
+
+        def run(kind, step):
+            for fn in jobs.get((kind, step), []):
+                fn()
+
+        def piece(copy, key, src, n_):
+            if key not in grps:
+                grps[key] = new_grp()
+            cols = slice(n_ * 256, (n_ + 1) * 256)
+            regroup(copy, grps[key][:, cols, :], src[:, :, cols])
+
+        def uo_piece(g, hf, n_):
+            piece(scopy, ("uo", g, hf), uo_raw[:, g, :, hf * HALF : (hf + 1) * HALF], n_)
+
+        def uo_quant(g, hf):
+            cols = slice(hf * HALF, (hf + 1) * HALF)
+            quant(grps[("uo", g, hf)][:], uo_codes[:, g, cols], uo_scales[:, g, cols])
+
+        def t3_piece(copy, c, g, n_):
+            piece(copy, ("t3", c, g), t3s[c * 2 + g][:], n_)
+
+        def t3_quant(c, g):
+            quant(grps[("t3", c, g)][:], t3_codes[:, c, g, :], t3_scales[:, c, g, :])
+
+        def x1_regroup(hf):
+            grps[("x1", hf)] = new_grp()
+            regroup(vcopy, grps[("x1", hf)][:], x_raw[:, 1, :, hf * HALF : (hf + 1) * HALF])
+
+        def x1_quant(hf):
+            cols = slice(hf * HALF, (hf + 1) * HALF)
+            quant(grps[("x1", hf)][:], x_codes[:, 1, cols], x_scales[:, 1, cols])
+
+        def pe_pass(c, k, g):
+            if g == 0:
+                accs[(c, k)] = ps.tile([P, HALF], F32, name="bank")
+            cc = slice(k * P, (k + 1) * P)
+            mx(accs[(c, k)][:], uo_codes[:, g, cc], uo_scales[:, g, cc], t3_codes[:, c, g, :], t3_scales[:, c, g, :], g == 0, g == 1)
+
+        def pe_group(c, k):
+            pe_pass(c, k, 0)
+            pe_pass(c, k, 1)
+
+        def evac(c, k, on_vector):
+            osb = o_pool.tile([P, HALF], F32, name="osb")
+            if on_vector:
+                nc.vector.tensor_scalar(out=osb[:], in0=accs[(c, k)][:], scalar1=biasf[:, k : k + 1], scalar2=None, op0=ADD)
+            else:
+                nc.scalar.activation(out=osb[:], in_=accs[(c, k)][:], func=IDENT, bias=biasf[:, k : k + 1], scale=1.0)
+            ov = out[c // 2].rearrange("(i m) h w d -> i m (h w d)", m=P)
+            nc.sync.dma_start(out=ov[k][:, (c % 2) * HALF : (c % 2 + 1) * HALF], in_=osb[:])
+
+        at("V", 0, lambda: quant(g_ui1[:], ui_codes[:, HALF:R], ui_scales[:, HALF:R]))
+        for n_, (g, hf, st) in enumerate(((0, 0, 4), (1, 0, 6), (0, 1, 10), (1, 1, 14))):
+            at("S", st, lambda g=g, hf=hf: uo_piece(g, hf, 0))
+            at("S", st + 1, lambda g=g, hf=hf: uo_piece(g, hf, 1))
+            at("V", st + 2, lambda g=g, hf=hf: uo_quant(g, hf))
+        for hf in range(2):
+            at("V", 9 + 2 * hf, lambda hf=hf: x1_regroup(hf))
+            at("V", 10 + 2 * hf, lambda hf=hf: x1_quant(hf))
+        at("S", 13, lambda: nc.scalar.copy(out=biasf[:], in_=bias_bf[:]))
+        for c in range(4):
+            for g in range(2):
+                if (c, g) != (3, 1):
+                    st = 8 * c + 4 * g + 8
+                    at("S", st, lambda c=c, g=g: t3_piece(scopy, c, g, 0))
+                    at("S", st + 1, lambda c=c, g=g: t3_piece(scopy, c, g, 1))
+                    at("V", st + 2, lambda c=c, g=g: t3_quant(c, g))
+        for c in range(3):
+            for k in range(8):
+                st = 8 * c + 15 + (k if c < 2 else k // 2)
+                at("PE", st, lambda c=c, k=k: pe_group(c, k))
+                at("E", st + 1, lambda c=c, k=k: evac(c, k, False))
+
+        for s in range(-1, NU + 4):
+            if valid(s + 1):
+                pe_t0(s + 1)
+            run("PE", s)
+            if valid(s - 1) and on_pe(s - 1):
+                pe_w(s - 1)
+            run("E", s)
+            if valid(s - 1) and not on_pe(s - 1):
+                s_wc(s - 1)
+            if valid(s - 3):
+                s_dc(s - 3)
+            if valid(s + 1):
+                s_hc(s + 1)
+            ops = [
+                v_h(s) if valid(s) else [],
+                v_w(s - 2) if valid(s - 2) and not on_pe(s - 2) else [],
+                v_d(s - 4) if valid(s - 4) else [],
+            ]
+            for n_ in range(2):
+                for lst in ops:
+                    if lst:
+                        lst[n_]()
+            run("V", s)
+            run("S", s)
+
+        for k in range(8):
+            pe_pass(3, k, 0)
+        t3_piece(scopy, 3, 1, 0)
+        t3_piece(vcopy, 3, 1, 1)
+        t3_quant(3, 1)
+        for k in range(8):
+            pe_pass(3, k, 1)
+            evac(3, k, k % 2 == 1)

@@ -43,7 +43,7 @@ def tile_lowrankconv3d_pa_kernel(tc, x, U_k_h, U_k_w, U_k_d, U_c_in, U_c_out, bi
         t3_pool = ctx.enter_context(tc.tile_pool(name="t3p", bufs=3))
         o_pool = ctx.enter_context(tc.tile_pool(name="op", bufs=8))
         ps = ctx.enter_context(tc.psum_pool(name="ps", bufs=8))
-        ctx.enter_context(tc.manual_schedule())
+        pass
 
         x_raw = keep.tile([P, B, 4, N], BF16, name="x_raw")
         ui_raw = keep.tile([P, 4, R], BF16, name="ui_raw")
@@ -179,10 +179,11 @@ def tile_lowrankconv3d_pa_kernel(tc, x, U_k_h, U_k_w, U_k_d, U_c_in, U_c_out, bi
             t2s[q] = t2_pool.tile([P, HALF], F32, name="t2")
             nc.scalar.activation(out=t2s[q][:], in_=t1s[q][:], func=COPY, scale=tap(1, 1, q % 8))
 
-        def pe_w(q):
-            t2s[q] = ps.tile([P, HALF], F32, name="bank")
+        def pe_w(q, taps):
+            if 0 in taps:
+                t2s[q] = ps.tile([P, HALF], F32, name="bank")
             n_ = PE_TILES.index(q % 8)
-            for k in range(3):
+            for k in taps:
                 nc.tensor.matmul(
                     out=rows(t2s[q][:], 0, 4),
                     lhsT=diag[:, 3 * n_ + k, :],
@@ -201,7 +202,7 @@ def tile_lowrankconv3d_pa_kernel(tc, x, U_k_h, U_k_w, U_k_d, U_c_in, U_c_out, bi
 
         def s_dc(q):
             key = q // 4
-            if q % 4 == 0:
+            if key not in t3s:
                 t3s[key] = t3_pool.tile([P, 4, HALF], F32, name="t3f")
             nc.scalar.activation(out=t3s[key][:, q % 4, :], in_=t2s[q][:], func=COPY, scale=tap(2, 1, q % 8))
 
@@ -296,19 +297,24 @@ def tile_lowrankconv3d_pa_kernel(tc, x, U_k_h, U_k_w, U_k_d, U_c_in, U_c_out, bi
             if valid(s + 1):
                 pe_t0(s + 1)
             run("PE", s)
+            if valid(s - 2) and on_pe(s - 2):
+                pe_w(s - 2, (1, 2))
             if valid(s - 1) and on_pe(s - 1):
-                pe_w(s - 1)
+                pe_w(s - 1, (0,))
             run("E", s)
             if valid(s - 1) and not on_pe(s - 1):
                 s_wc(s - 1)
-            if valid(s - 3):
+            if valid(s - 4) and on_pe(s - 4):
+                s_dc(s - 4)
+            if valid(s - 3) and not on_pe(s - 3):
                 s_dc(s - 3)
             if valid(s + 1):
                 s_hc(s + 1)
             ops = [
                 v_h(s) if valid(s) else [],
                 v_w(s - 2) if valid(s - 2) and not on_pe(s - 2) else [],
-                v_d(s - 4) if valid(s - 4) else [],
+                v_d(s - 5) if valid(s - 5) and on_pe(s - 5) else [],
+                v_d(s - 4) if valid(s - 4) and not on_pe(s - 4) else [],
             ]
             for n_ in range(2):
                 for lst in ops:

@@ -17,7 +17,9 @@ P = 128
 B, CI, R, CO, H, W, D = 2, 512, 1024, 1024, 8, 8, 16
 N = H * W * D
 HALF = 512
-NU = 32
+CHUNKS = ((0, 0, 4), (0, 4, 4), (1, 0, 4), (1, 4, 4))
+NC = len(CHUNKS)
+NU = 8 * NC
 PE_TILES = (1, 4, 6)
 FLOPS = 2 * B * N * (CI * R + R * CO) + 2 * 9 * B * R * N
 
@@ -30,7 +32,7 @@ def regroup(copy, dst, src):
 
 
 def rows(ap, r0, r1):
-    return ap.rearrange("p (h c) -> p h c", h=4)[:, r0:r1, :]
+    return ap.rearrange("p (h c) -> p h c", c=128)[:, r0:r1, :]
 
 
 def tile_lowrankconv3d_pa_kernel(tc, x, U_k_h, U_k_w, U_k_d, U_c_in, U_c_out, bias, out):
@@ -54,44 +56,38 @@ def tile_lowrankconv3d_pa_kernel(tc, x, U_k_h, U_k_w, U_k_d, U_c_in, U_c_out, bi
         ui_scales = keep.tile([P, R], U8, name="ui_scales", align_bytes=64)
         uo_codes = keep.tile([P, 2, CO], U32, name="uo_codes", align_bytes=64)
         uo_scales = keep.tile([P, 2, CO], U8, name="uo_scales", align_bytes=64)
-        t3_codes = keep.tile([P, 4, 2, HALF], U32, name="t3_codes", align_bytes=64)
-        t3_scales = keep.tile([P, 4, 2, HALF], U8, name="t3_scales", align_bytes=64)
-        tap_bf = keep.tile([P, 3, 8, 4], BF16, name="tap_bf")
-        tapf = keep.tile([P, 3, 8, 4], F32, name="tapf")
-        bias_bf = keep.tile([P, 8], BF16, name="bias_bf")
-        biasf = keep.tile([P, 8], F32, name="biasf")
+        t3_codes = keep.tile([P, NC, 2, HALF], U32, name="t3_codes", align_bytes=64)
+        t3_scales = keep.tile([P, NC, 2, HALF], U8, name="t3_scales", align_bytes=64)
+        vec_rows = keep.tile([P, R], BF16, name="vec_rows")
+        vecs = keep.tile([P, 8, 10], F32, name="vecs")
+        ident = keep.tile([P, P], BF16, name="ident")
         pads = [keep.tile([P, 4, 160], F32, name="t1pad%d" % k) for k in range(len(PE_TILES))]
-        if PE_TILES:
-            ident = keep.tile([P, P], F32, name="ident")
-            diag = keep.tile([P, 3 * len(PE_TILES), P], F32, name="diag")
-            make_identity(nc, ident[:])
-            for t in pads:
-                nc.gpsimd.memset(t[:], 0.0)
+        diag = keep.tile([P, 3 * len(PE_TILES), P], F32, name="diag")
+        nc.gpsimd.memset(vec_rows[:], 0.0)
+        make_identity(nc, ident[:])
+        for t in pads:
+            nc.gpsimd.memset(t[:], 0.0)
 
+        for f, u in enumerate((U_k_h, U_k_w, U_k_d)):
+            nc.scalar.dma_start(out=vec_rows[3 * f : 3 * f + 3, :], in_=u)
+        nc.scalar.dma_start(out=vec_rows[9:10, :], in_=bias.rearrange("(o c) -> o c", o=1))
         xv = [x[b].rearrange("(p t) h w d -> p t (h w d)", t=4) for b in range(B)]
         uiv = U_c_in.rearrange("(p t) r -> p t r", t=4)
-        uov = U_c_out.rearrange("(g p t) c -> g p t c", g=2, t=4)
-        nc.sync.dma_start(out=ui_raw[:, :, 0:HALF], in_=uiv[:, :, 0:HALF])
+        uov = U_c_out.rearrange("(g t p) c -> g p t c", g=2, t=4)
+        nc.sync.dma_start(out=ui_raw[:, :, 0:P], in_=uiv[:, :, 0:P])
         nc.sync.dma_start(out=x_raw[:, 0, :, 0:HALF], in_=xv[0][:, :, 0:HALF])
         nc.sync.dma_start(out=x_raw[:, 0, :, HALF:N], in_=xv[0][:, :, HALF:N])
+        nc.sync.dma_start(out=ui_raw[:, :, P:HALF], in_=uiv[:, :, P:HALF])
         nc.sync.dma_start(out=ui_raw[:, :, HALF:R], in_=uiv[:, :, HALF:R])
-        with nc.allow_non_contiguous_dma(reason="taps come in 8-byte runs"):
-            for f, u in enumerate((U_k_h, U_k_w, U_k_d)):
-                nc.sync.dma_start(
-                    out=tap_bf[:, f, 0:6, :],
-                    in_=u.rearrange("k r -> (k r)").rearrange("(q m j) -> m q j", q=6, m=P, j=4),
-                )
         nc.sync.dma_start(out=uo_raw[:, 0, :, :], in_=uov[0])
         nc.sync.dma_start(out=uo_raw[:, 1, :, :], in_=uov[1])
         nc.sync.dma_start(out=x_raw[:, 1, :, :], in_=xv[1])
-        with nc.allow_non_contiguous_dma(reason="bias: one element a partition"):
-            nc.sync.dma_start(out=bias_bf[:], in_=bias.rearrange("(i m) -> m i", i=8, m=P))
 
         vcopy = nc.vector.tensor_copy
         scopy = nc.scalar.copy
 
         def tap(f, k, tl):
-            return tapf[:, f, k * 2 + tl // 4, tl % 4 : tl % 4 + 1]
+            return vecs[:, tl, 3 * f + k : 3 * f + k + 1]
 
         def quant(src, codes, scales):
             nc.vector.quantize_mx(out=codes.bitcast(FP8X4), scales=scales, in_=src.rearrange("p w t -> p (w t)"))
@@ -102,34 +98,34 @@ def tile_lowrankconv3d_pa_kernel(tc, x, U_k_h, U_k_w, U_k_d, U_c_in, U_c_out, bi
         def stt(o, a, s, c):
             nc.vector.scalar_tensor_tensor(out=o, in0=a, scalar=s, in1=c, op0=MULT, op1=ADD)
 
-        def ui_regroup(copy, grp, g, j0, j1):
-            copy(
-                out=grp[:, j0 * P : j1 * P, :].rearrange("p (j m) t -> p j m t", j=j1 - j0),
-                in_=ui_raw[:, :, g * HALF : (g + 1) * HALF].rearrange("p t (m j) -> p j m t", j=4)[:, j0:j1],
-            )
+        def ui_regroup(copy, grp, g, lo, hi):
+            regroup(copy, grp[:, lo:hi, :], ui_raw[:, :, g * HALF + lo : g * HALF + hi])
 
         g_ui0 = new_grp()
         g_x00 = new_grp()
         g_x01 = new_grp()
         g_ui1 = new_grp()
-        ui_regroup(vcopy, g_ui0, 0, 0, 1)
-        ui_regroup(scopy, g_ui0, 0, 1, 4)
+        vec_ps = ps.tile([P, 8, P], BF16, name="bank")
+        for i in range(8):
+            nc.tensor.transpose(vec_ps[:, i, :], vec_rows[:, i * P : (i + 1) * P], ident[:])
+        nc.scalar.copy(out=vecs[:], in_=vec_ps[:, :, 0:10])
+        ui_regroup(vcopy, g_ui0, 0, 0, P)
         regroup(vcopy, g_x00[:], x_raw[:, 0, :, 0:HALF])
         quant(g_ui0[:, 0:P, :], ui_codes[:, 0:P], ui_scales[:, 0:P])
         quant(g_x00[:], x_codes[:, 0, 0:HALF], x_scales[:, 0, 0:HALF])
         regroup(vcopy, g_x01[:], x_raw[:, 0, :, HALF:N])
-        quant(g_ui0[:, P : 2 * P, :], ui_codes[:, P : 2 * P], ui_scales[:, P : 2 * P])
+        ui_regroup(scopy, g_ui0, 0, P, HALF)
         quant(g_x01[:], x_codes[:, 0, HALF:N], x_scales[:, 0, HALF:N])
+        quant(g_ui0[:, P : 2 * P, :], ui_codes[:, P : 2 * P], ui_scales[:, P : 2 * P])
         quant(g_ui0[:, 2 * P : 4 * P, :], ui_codes[:, 2 * P : 4 * P], ui_scales[:, 2 * P : 4 * P])
-        ui_regroup(scopy, g_ui1, 1, 0, 4)
-        nc.scalar.copy(out=tapf[:, :, 0:6, :], in_=tap_bf[:, :, 0:6, :])
+        ui_regroup(scopy, g_ui1, 1, 0, HALF)
         for n_, tl in enumerate(PE_TILES):
             for k in range(3):
                 nc.gpsimd.tensor_scalar(
                     out=diag[:, 3 * n_ + k, :], in0=ident[:], scalar1=tap(1, k, tl), scalar2=0.0, op0=MULT, op1=ADD
                 )
 
-        t0a, t0b, t1s, t2s, t3s = {}, {}, {}, {}, {}
+        t0s, t1s, t2s, t3s = {}, {}, {}, {}
 
         def valid(q):
             return 0 <= q < NU
@@ -142,14 +138,28 @@ def tile_lowrankconv3d_pa_kernel(tc, x, U_k_h, U_k_w, U_k_d, U_c_in, U_c_out, bi
                 out=o, lhsT=lc.bitcast(FP8X4), lhsT_scale=ls, rhs=rc.bitcast(FP8X4), rhs_scale=rs, start=start, stop=stop
             )
 
+        def geo(q):
+            b, h0, nh = CHUNKS[q // 8]
+            return b, h0, nh, nh * 128
+
         def pe_t0(q):
-            c, tl = q // 8, q % 8
-            b, hh = c // 2, c % 2
+            b, h0, nh, cw = geo(q)
+            tl = q % 8
             mc = slice(tl * P, (tl + 1) * P)
-            t0a[q] = ps.tile([P, HALF], F32, name="bank")
-            t0b[q] = ps.tile([P, HALF], F32, name="bank")
-            for t, lo in ((t0a[q], hh * HALF), (t0b[q], 128 + hh * 256)):
+            wins = [h0, h0 + 1 if h0 == 0 else h0 - 1] if nh == 4 else [min(h0 - 1, 4)]
+            banks = []
+            for w0 in wins:
+                t = ps.tile([P, HALF], F32, name="bank")
+                lo = w0 * 128
                 mx(t[:], ui_codes[:, mc], ui_scales[:, mc], x_codes[:, b, lo : lo + HALF], x_scales[:, b, lo : lo + HALF], True, True)
+                banks.append((t, w0))
+            t0s[q] = banks
+
+        def t0rows(q, r0, r1):
+            for t, w0 in t0s[q]:
+                if w0 <= r0 and r1 <= w0 + 4:
+                    return rows(t[:], r0 - w0, r1 - w0)
+            return None
 
         def t1rows(q, r0, r1):
             if on_pe(q):
@@ -157,53 +167,54 @@ def tile_lowrankconv3d_pa_kernel(tc, x, U_k_h, U_k_w, U_k_d, U_c_in, U_c_out, bi
             return rows(t1s[q][:], r0, r1)
 
         def s_hc(q):
+            b, h0, nh, cw = geo(q)
             if on_pe(q):
                 t1s[q] = pads[PE_TILES.index(q % 8)]
             else:
-                t1s[q] = t1_pool.tile([P, HALF], F32, name="t1")
-            nc.scalar.activation(out=t1rows(q, 0, 4), in_=rows(t0a[q][:], 0, 4), func=COPY, scale=tap(0, 1, q % 8))
+                t1s[q] = t1_pool.tile([P, cw], F32, name="t1")
+            nc.scalar.activation(out=t1rows(q, 0, nh), in_=t0rows(q, h0, h0 + nh), func=COPY, scale=tap(0, 1, q % 8))
 
         def v_h(q):
-            tl, hh = q % 8, (q // 8) % 2
-            if hh == 0:
-                return [
-                    lambda: stt(t1rows(q, 1, 4), rows(t0a[q][:], 0, 3), tap(0, 0, tl), t1rows(q, 1, 4)),
-                    lambda: stt(t1rows(q, 0, 4), rows(t0b[q][:], 0, 4), tap(0, 2, tl), t1rows(q, 0, 4)),
-                ]
+            b, h0, nh, cw = geo(q)
+            tl = q % 8
+            lo = 1 if h0 == 0 else 0
+            hi = nh - 1 if h0 + nh == H else nh
             return [
-                lambda: stt(t1rows(q, 0, 4), rows(t0b[q][:], 0, 4), tap(0, 0, tl), t1rows(q, 0, 4)),
-                lambda: stt(t1rows(q, 0, 3), rows(t0a[q][:], 1, 4), tap(0, 2, tl), t1rows(q, 0, 3)),
+                lambda: stt(t1rows(q, lo, nh), t0rows(q, h0 + lo - 1, h0 + nh - 1), tap(0, 0, tl), t1rows(q, lo, nh)),
+                lambda: stt(t1rows(q, 0, hi), t0rows(q, h0 + 1, h0 + hi + 1), tap(0, 2, tl), t1rows(q, 0, hi)),
             ]
 
         def s_wc(q):
-            t2s[q] = t2_pool.tile([P, HALF], F32, name="t2")
+            t2s[q] = t2_pool.tile([P, geo(q)[3]], F32, name="t2")
             nc.scalar.activation(out=t2s[q][:], in_=t1s[q][:], func=COPY, scale=tap(1, 1, q % 8))
 
         def pe_w(q, taps):
+            nh, cw = geo(q)[2:4]
             if 0 in taps:
-                t2s[q] = ps.tile([P, HALF], F32, name="bank")
+                bank = ps.tile([P, HALF], F32, name="bank")
+                t2s[q] = bank[:, 0:cw]
             n_ = PE_TILES.index(q % 8)
             for k in taps:
                 nc.tensor.matmul(
-                    out=rows(t2s[q][:], 0, 4),
+                    out=rows(t2s[q][:], 0, nh),
                     lhsT=diag[:, 3 * n_ + k, :],
-                    rhs=t1s[q][:, :, 16 * k : 16 * k + 128],
+                    rhs=t1s[q][:, 0:nh, 16 * k : 16 * k + 128],
                     start=(k == 0),
                     stop=(k == 2),
                 )
 
         def v_w(q):
-            tl = q % 8
-            a, o = rows(t1s[q][:], 0, 4), rows(t2s[q][:], 0, 4)
+            tl, nh = q % 8, geo(q)[2]
+            a, o = rows(t1s[q][:], 0, nh), rows(t2s[q][:], 0, nh)
             return [
                 lambda: stt(o[:, :, 16:128], a[:, :, 0:112], tap(1, 0, tl), o[:, :, 16:128]),
                 lambda: stt(o[:, :, 0:112], a[:, :, 16:128], tap(1, 2, tl), o[:, :, 0:112]),
             ]
 
         def s_dc(q):
-            key = q // 4
+            key, cw = q // 4, geo(q)[3]
             if key not in t3s:
-                t3s[key] = t3_pool.tile([P, 4, HALF], F32, name="t3f")
+                t3s[key] = t3_pool.tile([P, 4, cw], F32, name="t3f")
             nc.scalar.activation(out=t3s[key][:, q % 4, :], in_=t2s[q][:], func=COPY, scale=tap(2, 1, q % 8))
 
         def v_d(q):
@@ -225,24 +236,27 @@ def tile_lowrankconv3d_pa_kernel(tc, x, U_k_h, U_k_w, U_k_d, U_c_in, U_c_out, bi
             for fn in jobs.get((kind, step), []):
                 fn()
 
-        def piece(copy, key, src, n_):
+        def piece(copy, key, src, lo, hi):
             if key not in grps:
                 grps[key] = new_grp()
-            cols = slice(n_ * 256, (n_ + 1) * 256)
-            regroup(copy, grps[key][:, cols, :], src[:, :, cols])
+            regroup(copy, grps[key][:, lo:hi, :], src[:, :, lo:hi])
 
         def uo_piece(g, hf, n_):
-            piece(scopy, ("uo", g, hf), uo_raw[:, g, :, hf * HALF : (hf + 1) * HALF], n_)
+            piece(scopy, ("uo", g, hf), uo_raw[:, g, :, hf * HALF : (hf + 1) * HALF], n_ * 256, (n_ + 1) * 256)
 
         def uo_quant(g, hf):
             cols = slice(hf * HALF, (hf + 1) * HALF)
             quant(grps[("uo", g, hf)][:], uo_codes[:, g, cols], uo_scales[:, g, cols])
 
-        def t3_piece(copy, c, g, n_):
-            piece(copy, ("t3", c, g), t3s[c * 2 + g][:], n_)
+        def t3_piece(copy, c, g, lo, hi):
+            piece(copy, ("t3", c, g), t3s[c * 2 + g][:], lo, hi)
+
+        def width(c):
+            return CHUNKS[c][2] * 128
 
         def t3_quant(c, g):
-            quant(grps[("t3", c, g)][:], t3_codes[:, c, g, :], t3_scales[:, c, g, :])
+            cw = width(c)
+            quant(grps[("t3", c, g)][:, 0:cw, :], t3_codes[:, c, g, 0:cw], t3_scales[:, c, g, 0:cw])
 
         def x1_regroup(hf):
             grps[("x1", hf)] = new_grp()
@@ -256,20 +270,23 @@ def tile_lowrankconv3d_pa_kernel(tc, x, U_k_h, U_k_w, U_k_d, U_c_in, U_c_out, bi
             if g == 0:
                 accs[(c, k)] = ps.tile([P, HALF], F32, name="bank")
             cc = slice(k * P, (k + 1) * P)
-            mx(accs[(c, k)][:], uo_codes[:, g, cc], uo_scales[:, g, cc], t3_codes[:, c, g, :], t3_scales[:, c, g, :], g == 0, g == 1)
+            cw = width(c)
+            mx(accs[(c, k)][:, 0:cw], uo_codes[:, g, cc], uo_scales[:, g, cc], t3_codes[:, c, g, 0:cw], t3_scales[:, c, g, 0:cw], g == 0, g == 1)
 
         def pe_group(c, k):
             pe_pass(c, k, 0)
             pe_pass(c, k, 1)
 
         def evac(c, k, on_vector):
-            osb = o_pool.tile([P, HALF], F32, name="osb")
+            b, h0, nh = CHUNKS[c]
+            cw = width(c)
+            osb = o_pool.tile([P, cw], F32, name="osb")
             if on_vector:
-                nc.vector.tensor_scalar(out=osb[:], in0=accs[(c, k)][:], scalar1=biasf[:, k : k + 1], scalar2=None, op0=ADD)
+                nc.vector.tensor_scalar(out=osb[:], in0=accs[(c, k)][:, 0:cw], scalar1=vecs[:, k, 9:10], scalar2=None, op0=ADD)
             else:
-                nc.scalar.activation(out=osb[:], in_=accs[(c, k)][:], func=IDENT, bias=biasf[:, k : k + 1], scale=1.0)
-            ov = out[c // 2].rearrange("(i m) h w d -> i m (h w d)", m=P)
-            nc.sync.dma_start(out=ov[k][:, (c % 2) * HALF : (c % 2 + 1) * HALF], in_=osb[:])
+                nc.scalar.activation(out=osb[:], in_=accs[(c, k)][:, 0:cw], func=IDENT, bias=vecs[:, k, 9:10], scale=1.0)
+            ov = out[b].rearrange("(i m) h w d -> i m (h w d)", m=P)
+            nc.sync.dma_start(out=ov[k][:, h0 * 128 : h0 * 128 + cw], in_=osb[:])
 
         at("V", 0, lambda: quant(g_ui1[:], ui_codes[:, HALF:R], ui_scales[:, HALF:R]))
         for n_, (g, hf, st) in enumerate(((0, 0, 4), (1, 0, 6), (0, 1, 10), (1, 1, 14))):
@@ -279,17 +296,17 @@ def tile_lowrankconv3d_pa_kernel(tc, x, U_k_h, U_k_w, U_k_d, U_c_in, U_c_out, bi
         for hf in range(2):
             at("V", 9 + 2 * hf, lambda hf=hf: x1_regroup(hf))
             at("V", 10 + 2 * hf, lambda hf=hf: x1_quant(hf))
-        at("S", 13, lambda: nc.scalar.copy(out=biasf[:], in_=bias_bf[:]))
-        for c in range(4):
+        for c in range(NC):
             for g in range(2):
-                if (c, g) != (3, 1):
+                if (c, g) != (NC - 1, 1):
                     st = 8 * c + 4 * g + 8
-                    at("S", st, lambda c=c, g=g: t3_piece(scopy, c, g, 0))
-                    at("S", st + 1, lambda c=c, g=g: t3_piece(scopy, c, g, 1))
+                    at("S", st, lambda c=c, g=g: t3_piece(scopy, c, g, 0, 256))
+                    if width(c) > 256:
+                        at("S", st + 1, lambda c=c, g=g: t3_piece(scopy, c, g, 256, 512))
                     at("V", st + 2, lambda c=c, g=g: t3_quant(c, g))
-        for c in range(3):
+        for c in range(NC - 1):
             for k in range(8):
-                st = 8 * c + 15 + (k if c < 2 else k // 2)
+                st = 8 * c + 15 + (k if c < NC - 2 else k // 2)
                 at("PE", st, lambda c=c, k=k: pe_group(c, k))
                 at("E", st + 1, lambda c=c, k=k: evac(c, k, False))
 
@@ -323,11 +340,12 @@ def tile_lowrankconv3d_pa_kernel(tc, x, U_k_h, U_k_w, U_k_d, U_c_in, U_c_out, bi
             run("V", s)
             run("S", s)
 
+        last = NC - 1
         for k in range(8):
-            pe_pass(3, k, 0)
-        t3_piece(scopy, 3, 1, 0)
-        t3_piece(vcopy, 3, 1, 1)
-        t3_quant(3, 1)
+            pe_pass(last, k, 0)
+        t3_piece(scopy, last, 1, 0, width(last) // 2)
+        t3_piece(vcopy, last, 1, width(last) // 2, width(last))
+        t3_quant(last, 1)
         for k in range(8):
-            pe_pass(3, k, 1)
-            evac(3, k, k % 2 == 1)
+            pe_pass(last, k, 1)
+            evac(last, k, k % 2 == 1)

@@ -63,10 +63,10 @@ def tile_lowrankconv3d_pa_kernel(tc, x, U_k_h, U_k_w, U_k_d, U_c_in, U_c_out, bi
         ident = keep.tile([P, P], BF16, name="ident")
         pads = [keep.tile([P, 4, 160], F32, name="t1pad%d" % k) for k in range(len(PE_TILES))]
         diag = keep.tile([P, 3 * len(PE_TILES), P], F32, name="diag")
-        nc.gpsimd.memset(vec_rows[:], 0.0)
+        nc.vector.memset(vec_rows[:], 0.0)
         make_identity(nc, ident[:])
         for t in pads:
-            nc.gpsimd.memset(t[:], 0.0)
+            nc.vector.memset(t[:], 0.0)
 
         for f, u in enumerate((U_k_h, U_k_w, U_k_d)):
             nc.scalar.dma_start(out=vec_rows[3 * f : 3 * f + 3, :], in_=u)
@@ -109,6 +109,9 @@ def tile_lowrankconv3d_pa_kernel(tc, x, U_k_h, U_k_w, U_k_d, U_c_in, U_c_out, bi
         for i in range(8):
             nc.tensor.transpose(vec_ps[:, i, :], vec_rows[:, i * P : (i + 1) * P], ident[:])
         nc.scalar.copy(out=vecs[:], in_=vec_ps[:, :, 0:10])
+        for n_, tl in enumerate(PE_TILES):
+            for k in range(3):
+                nc.scalar.activation(out=diag[:, 3 * n_ + k, :], in_=ident[:], func=COPY, scale=tap(1, k, tl))
         ui_regroup(vcopy, g_ui0, 0, 0, P)
         regroup(vcopy, g_x00[:], x_raw[:, 0, :, 0:HALF])
         quant(g_ui0[:, 0:P, :], ui_codes[:, 0:P], ui_scales[:, 0:P])
@@ -119,12 +122,6 @@ def tile_lowrankconv3d_pa_kernel(tc, x, U_k_h, U_k_w, U_k_d, U_c_in, U_c_out, bi
         quant(g_ui0[:, P : 2 * P, :], ui_codes[:, P : 2 * P], ui_scales[:, P : 2 * P])
         quant(g_ui0[:, 2 * P : 4 * P, :], ui_codes[:, 2 * P : 4 * P], ui_scales[:, 2 * P : 4 * P])
         ui_regroup(scopy, g_ui1, 1, 0, HALF)
-        for n_, tl in enumerate(PE_TILES):
-            for k in range(3):
-                nc.gpsimd.tensor_scalar(
-                    out=diag[:, 3 * n_ + k, :], in0=ident[:], scalar1=tap(1, k, tl), scalar2=0.0, op0=MULT, op1=ADD
-                )
-
         t0s, t1s, t2s, t3s = {}, {}, {}, {}
 
         def valid(q):
@@ -260,7 +257,7 @@ def tile_lowrankconv3d_pa_kernel(tc, x, U_k_h, U_k_w, U_k_d, U_c_in, U_c_out, bi
 
         def x1_regroup(hf):
             grps[("x1", hf)] = new_grp()
-            regroup(vcopy, grps[("x1", hf)][:], x_raw[:, 1, :, hf * HALF : (hf + 1) * HALF])
+            regroup(scopy, grps[("x1", hf)][:], x_raw[:, 1, :, hf * HALF : (hf + 1) * HALF])
 
         def x1_quant(hf):
             cols = slice(hf * HALF, (hf + 1) * HALF)
@@ -294,7 +291,7 @@ def tile_lowrankconv3d_pa_kernel(tc, x, U_k_h, U_k_w, U_k_d, U_c_in, U_c_out, bi
             at("S", st + 1, lambda g=g, hf=hf: uo_piece(g, hf, 1))
             at("V", st + 2, lambda g=g, hf=hf: uo_quant(g, hf))
         for hf in range(2):
-            at("V", 9 + 2 * hf, lambda hf=hf: x1_regroup(hf))
+            at("S", 9 + 2 * hf, lambda hf=hf: x1_regroup(hf))
             at("V", 10 + 2 * hf, lambda hf=hf: x1_quant(hf))
         for c in range(NC):
             for g in range(2):

@@ -11,16 +11,22 @@ FP8X4 = mybir.dt.float8_e4m3fn_x4
 MULT = mybir.AluOpType.mult
 ADD = mybir.AluOpType.add
 COPY = mybir.ActivationFunctionType.Copy
-IDENT = mybir.ActivationFunctionType.Identity
+IDENTITY = mybir.ActivationFunctionType.Identity
 
 P = 128
+PACK = 4
 B, CI, R, CO, H, W, D = 2, 512, 1024, 1024, 8, 8, 16
 N = H * W * D
-HALF = 512
-CHUNKS = ((0, 0, 4), (0, 4, 4), (1, 0, 4), (1, 4, 4))
-NC = len(CHUNKS)
-NU = 8 * NC
-PE_TILES = (1, 4, 6)
+ROW = W * D
+CHUNK_ROWS = 4
+CHUNK = CHUNK_ROWS * ROW
+CHUNKS = B * N // CHUNK
+TILES = R // P
+PASS_TILES = PACK
+PADDED_ROW = ROW + 2 * D
+TENSOR_TILES = (1, 4, 6)
+UNITS = CHUNKS * TILES
+PASSES = 2 * CHUNKS
 FLOPS = 2 * B * N * (CI * R + R * CO) + 2 * 9 * B * R * N
 
 
@@ -31,318 +37,290 @@ def regroup(copy, dst, src):
     )
 
 
-def rows(ap, r0, r1):
-    return ap.rearrange("p (h c) -> p h c", c=128)[:, r0:r1, :]
+def by_rows(ap):
+    return ap.rearrange("p (h c) -> p h c", c=ROW)
+
+
+def by_depth(ap):
+    return ap.rearrange("p (r d) -> p r d", d=D)
 
 
 def tile_lowrankconv3d_pa_kernel(tc, x, U_k_h, U_k_w, U_k_d, U_c_in, U_c_out, bias, out):
     nc = tc.nc
     with ExitStack() as ctx:
         keep = ctx.enter_context(tc.tile_pool(name="keep", bufs=1))
-        grp_pool = ctx.enter_context(tc.tile_pool(name="grp", bufs=4))
-        t1_pool = ctx.enter_context(tc.tile_pool(name="t1p", bufs=6))
-        t2_pool = ctx.enter_context(tc.tile_pool(name="t2p", bufs=6))
-        t3_pool = ctx.enter_context(tc.tile_pool(name="t3p", bufs=3))
-        o_pool = ctx.enter_context(tc.tile_pool(name="op", bufs=8))
-        ps = ctx.enter_context(tc.psum_pool(name="ps", bufs=8))
-        pass
+        grouped_pool = ctx.enter_context(tc.tile_pool(name="grouped", bufs=4))
+        t1_pool = ctx.enter_context(tc.tile_pool(name="t1", bufs=6))
+        t2_pool = ctx.enter_context(tc.tile_pool(name="t2", bufs=6))
+        t3_pool = ctx.enter_context(tc.tile_pool(name="t3", bufs=3))
+        out_pool = ctx.enter_context(tc.tile_pool(name="out", bufs=8))
+        banks = ctx.enter_context(tc.psum_pool(name="banks", bufs=8))
 
-        x_raw = keep.tile([P, B, 4, N], BF16, name="x_raw")
-        ui_raw = keep.tile([P, 4, R], BF16, name="ui_raw")
-        uo_raw = keep.tile([P, 2, 4, CO], BF16, name="uo_raw")
+        x_raw = keep.tile([P, B, PACK, N], BF16, name="x_raw")
+        ui_raw = keep.tile([P, PACK, R], BF16, name="ui_raw")
+        uo_raw = keep.tile([P, 2, PACK, CO], BF16, name="uo_raw")
         x_codes = keep.tile([P, B, N], U32, name="x_codes", align_bytes=64)
         x_scales = keep.tile([P, B, N], U8, name="x_scales", align_bytes=64)
         ui_codes = keep.tile([P, R], U32, name="ui_codes", align_bytes=64)
         ui_scales = keep.tile([P, R], U8, name="ui_scales", align_bytes=64)
         uo_codes = keep.tile([P, 2, CO], U32, name="uo_codes", align_bytes=64)
         uo_scales = keep.tile([P, 2, CO], U8, name="uo_scales", align_bytes=64)
-        t3_codes = keep.tile([P, NC, 2, HALF], U32, name="t3_codes", align_bytes=64)
-        t3_scales = keep.tile([P, NC, 2, HALF], U8, name="t3_scales", align_bytes=64)
+        t3_codes = keep.tile([P, CHUNKS, 2, CHUNK], U32, name="t3_codes", align_bytes=64)
+        t3_scales = keep.tile([P, CHUNKS, 2, CHUNK], U8, name="t3_scales", align_bytes=64)
         vec_rows = keep.tile([P, R], BF16, name="vec_rows")
-        vecs = keep.tile([P, 8, 10], F32, name="vecs")
+        vecs = keep.tile([P, TILES, 10], F32, name="vecs")
         ident = keep.tile([P, P], BF16, name="ident")
-        pads = [keep.tile([P, 4, 160], F32, name="t1pad%d" % k) for k in range(len(PE_TILES))]
-        diag = keep.tile([P, 3 * len(PE_TILES), P], F32, name="diag")
+        diag = keep.tile([P, len(TENSOR_TILES), 3, P], F32, name="diag")
+        padded = [keep.tile([P, CHUNK_ROWS, PADDED_ROW], F32, name="padded%d" % i) for i in range(len(TENSOR_TILES))]
+
         nc.vector.memset(vec_rows[:], 0.0)
         make_identity(nc, ident[:])
-        for t in pads:
+        for t in padded:
             nc.vector.memset(t[:], 0.0)
 
         for f, u in enumerate((U_k_h, U_k_w, U_k_d)):
             nc.scalar.dma_start(out=vec_rows[3 * f : 3 * f + 3, :], in_=u)
         nc.scalar.dma_start(out=vec_rows[9:10, :], in_=bias.rearrange("(o c) -> o c", o=1))
-        xv = [x[b].rearrange("(p t) h w d -> p t (h w d)", t=4) for b in range(B)]
-        uiv = U_c_in.rearrange("(p t) r -> p t r", t=4)
-        uov = U_c_out.rearrange("(g t p) c -> g p t c", g=2, t=4)
-        nc.sync.dma_start(out=ui_raw[:, :, 0:P], in_=uiv[:, :, 0:P])
-        nc.sync.dma_start(out=x_raw[:, 0, :, 0:HALF], in_=xv[0][:, :, 0:HALF])
-        nc.sync.dma_start(out=x_raw[:, 0, :, HALF:N], in_=xv[0][:, :, HALF:N])
-        nc.sync.dma_start(out=ui_raw[:, :, P:HALF], in_=uiv[:, :, P:HALF])
-        nc.sync.dma_start(out=ui_raw[:, :, HALF:R], in_=uiv[:, :, HALF:R])
-        nc.sync.dma_start(out=uo_raw[:, 0, :, :], in_=uov[0])
-        nc.sync.dma_start(out=uo_raw[:, 1, :, :], in_=uov[1])
-        nc.sync.dma_start(out=x_raw[:, 1, :, :], in_=xv[1])
+        x_view = [x[b].rearrange("(p t) h w d -> p t (h w d)", t=PACK) for b in range(B)]
+        ui_view = U_c_in.rearrange("(p t) r -> p t r", t=PACK)
+        uo_view = U_c_out.rearrange("(g t p) c -> g p t c", g=2, t=PACK)
+        nc.sync.dma_start(out=ui_raw[:, :, 0:P], in_=ui_view[:, :, 0:P])
+        nc.sync.dma_start(out=x_raw[:, 0, :, 0:CHUNK], in_=x_view[0][:, :, 0:CHUNK])
+        nc.sync.dma_start(out=x_raw[:, 0, :, CHUNK:N], in_=x_view[0][:, :, CHUNK:N])
+        nc.sync.dma_start(out=ui_raw[:, :, P:512], in_=ui_view[:, :, P:512])
+        nc.sync.dma_start(out=ui_raw[:, :, 512:R], in_=ui_view[:, :, 512:R])
+        nc.sync.dma_start(out=uo_raw[:, 0, :, :], in_=uo_view[0])
+        nc.sync.dma_start(out=uo_raw[:, 1, :, :], in_=uo_view[1])
+        nc.sync.dma_start(out=x_raw[:, 1, :, :], in_=x_view[1])
 
-        vcopy = nc.vector.tensor_copy
-        scopy = nc.scalar.copy
+        on_vector = nc.vector.tensor_copy
+        on_scalar = nc.scalar.copy
 
-        def tap(f, k, tl):
-            return vecs[:, tl, 3 * f + k : 3 * f + k + 1]
+        def new_grouped():
+            return grouped_pool.tile([P, 512, PACK], BF16, name="grouped", align_bytes=64)
 
-        def quant(src, codes, scales):
-            nc.vector.quantize_mx(out=codes.bitcast(FP8X4), scales=scales, in_=src.rearrange("p w t -> p (w t)"))
+        def quantise(grouped, codes, scales):
+            nc.vector.quantize_mx(out=codes.bitcast(FP8X4), scales=scales, in_=grouped.rearrange("p w t -> p (w t)"))
 
-        def new_grp():
-            return grp_pool.tile([P, HALF, 4], BF16, name="grp", align_bytes=64)
-
-        def stt(o, a, s, c):
-            nc.vector.scalar_tensor_tensor(out=o, in0=a, scalar=s, in1=c, op0=MULT, op1=ADD)
-
-        def ui_regroup(copy, grp, g, lo, hi):
-            regroup(copy, grp[:, lo:hi, :], ui_raw[:, :, g * HALF + lo : g * HALF + hi])
-
-        g_ui0 = new_grp()
-        g_x00 = new_grp()
-        g_x01 = new_grp()
-        g_ui1 = new_grp()
-        vec_ps = ps.tile([P, 8, P], BF16, name="bank")
-        for i in range(8):
-            nc.tensor.transpose(vec_ps[:, i, :], vec_rows[:, i * P : (i + 1) * P], ident[:])
-        nc.scalar.copy(out=vecs[:], in_=vec_ps[:, :, 0:10])
-        for n_, tl in enumerate(PE_TILES):
-            for k in range(3):
-                nc.scalar.activation(out=diag[:, 3 * n_ + k, :], in_=ident[:], func=COPY, scale=tap(1, k, tl))
-        ui_regroup(vcopy, g_ui0, 0, 0, P)
-        regroup(vcopy, g_x00[:], x_raw[:, 0, :, 0:HALF])
-        quant(g_ui0[:, 0:P, :], ui_codes[:, 0:P], ui_scales[:, 0:P])
-        quant(g_x00[:], x_codes[:, 0, 0:HALF], x_scales[:, 0, 0:HALF])
-        regroup(vcopy, g_x01[:], x_raw[:, 0, :, HALF:N])
-        ui_regroup(scopy, g_ui0, 0, P, HALF)
-        quant(g_x01[:], x_codes[:, 0, HALF:N], x_scales[:, 0, HALF:N])
-        quant(g_ui0[:, P : 2 * P, :], ui_codes[:, P : 2 * P], ui_scales[:, P : 2 * P])
-        quant(g_ui0[:, 2 * P : 4 * P, :], ui_codes[:, 2 * P : 4 * P], ui_scales[:, 2 * P : 4 * P])
-        ui_regroup(scopy, g_ui1, 1, 0, HALF)
-        t0s, t1s, t2s, t3s = {}, {}, {}, {}
-
-        def valid(q):
-            return 0 <= q < NU
-
-        def on_pe(q):
-            return (q % 8) in PE_TILES
-
-        def mx(o, lc, ls, rc, rs, start, stop):
+        def mx(acc, w_codes, w_scales, m_codes, m_scales, start, stop):
             nc.tensor.matmul_mx(
-                out=o, lhsT=lc.bitcast(FP8X4), lhsT_scale=ls, rhs=rc.bitcast(FP8X4), rhs_scale=rs, start=start, stop=stop
+                out=acc,
+                lhsT=w_codes.bitcast(FP8X4),
+                lhsT_scale=w_scales,
+                rhs=m_codes.bitcast(FP8X4),
+                rhs_scale=m_scales,
+                start=start,
+                stop=stop,
             )
 
-        def geo(q):
-            b, h0, nh = CHUNKS[q // 8]
-            return b, h0, nh, nh * 128
+        def tap(axis, k, tl):
+            return vecs[:, tl, 3 * axis + k : 3 * axis + k + 1]
 
-        def pe_t0(q):
-            b, h0, nh, cw = geo(q)
-            tl = q % 8
-            mc = slice(tl * P, (tl + 1) * P)
-            wins = [h0, h0 + 1 if h0 == 0 else h0 - 1] if nh == 4 else [min(h0 - 1, 4)]
-            banks = []
-            for w0 in wins:
-                t = ps.tile([P, HALF], F32, name="bank")
-                lo = w0 * 128
-                mx(t[:], ui_codes[:, mc], ui_scales[:, mc], x_codes[:, b, lo : lo + HALF], x_scales[:, b, lo : lo + HALF], True, True)
-                banks.append((t, w0))
-            t0s[q] = banks
+        def centre(dst, src, axis, tl):
+            nc.scalar.activation(out=dst, in_=src, func=COPY, scale=tap(axis, 1, tl))
 
-        def t0rows(q, r0, r1):
-            for t, w0 in t0s[q]:
-                if w0 <= r0 and r1 <= w0 + 4:
-                    return rows(t[:], r0 - w0, r1 - w0)
-            return None
+        def add_tap(acc, src, axis, k, tl):
+            nc.vector.scalar_tensor_tensor(out=acc, in0=src, scalar=tap(axis, k, tl), in1=acc, op0=MULT, op1=ADD)
 
-        def t1rows(q, r0, r1):
-            if on_pe(q):
-                return t1s[q][:, r0:r1, 16:144]
-            return rows(t1s[q][:], r0, r1)
+        vec_bank = banks.tile([P, TILES, P], BF16, name="bank")
+        for i in range(TILES):
+            nc.tensor.transpose(vec_bank[:, i, :], vec_rows[:, i * P : (i + 1) * P], ident[:])
+        nc.scalar.copy(out=vecs[:], in_=vec_bank[:, :, 0:10])
+        for i, tl in enumerate(TENSOR_TILES):
+            for k in range(3):
+                nc.scalar.activation(out=diag[:, i, k, :], in_=ident[:], func=COPY, scale=tap(1, k, tl))
 
-        def s_hc(q):
-            b, h0, nh, cw = geo(q)
-            if on_pe(q):
-                t1s[q] = pads[PE_TILES.index(q % 8)]
+        def prepare_ui(copy, grouped, lo, hi):
+            regroup(copy, grouped[:, lo % 512 : (hi - 1) % 512 + 1, :], ui_raw[:, :, lo:hi])
+
+        def quantise_ui(grouped, lo, hi):
+            quantise(grouped[:, lo % 512 : (hi - 1) % 512 + 1, :], ui_codes[:, lo:hi], ui_scales[:, lo:hi])
+
+        def prepare_x(copy, b, half):
+            cols = slice(half * 512, (half + 1) * 512)
+            grouped = new_grouped()
+            regroup(copy, grouped[:], x_raw[:, b, :, cols])
+            return grouped
+
+        def quantise_x(grouped, b, half):
+            cols = slice(half * 512, (half + 1) * 512)
+            quantise(grouped[:], x_codes[:, b, cols], x_scales[:, b, cols])
+
+        ui_lo = new_grouped()
+        prepare_ui(on_vector, ui_lo, 0, P)
+        x00 = prepare_x(on_vector, 0, 0)
+        quantise_ui(ui_lo, 0, P)
+        quantise_x(x00, 0, 0)
+        x01 = prepare_x(on_vector, 0, 1)
+        prepare_ui(on_scalar, ui_lo, P, 512)
+        quantise_x(x01, 0, 1)
+        quantise_ui(ui_lo, P, 2 * P)
+        quantise_ui(ui_lo, 2 * P, 512)
+        ui_hi = new_grouped()
+
+
+        own_bank, shifted_bank, t1_of, t2_of, t3_of, grouped_of, acc_of = {}, {}, {}, {}, {}, {}, {}
+
+        def is_unit(q):
+            return 0 <= q < UNITS
+
+        def on_tensor(q):
+            return q % TILES in TENSOR_TILES
+
+        def first_row(q):
+            return (q // TILES * CHUNK_ROWS) % H
+
+        def first_matmul(q):
+            b, h0, tl = q // TILES * CHUNK // N, first_row(q), q % TILES
+            w_cols = slice(tl * P, (tl + 1) * P)
+            own_bank[q] = banks.tile([P, CHUNK], F32, name="bank")
+            shifted_bank[q] = banks.tile([P, CHUNK], F32, name="bank")
+            for bank, row in ((own_bank[q], h0), (shifted_bank[q], h0 + 1 if h0 == 0 else h0 - 1)):
+                cols = slice(row * ROW, row * ROW + CHUNK)
+                mx(bank[:], ui_codes[:, w_cols], ui_scales[:, w_cols], x_codes[:, b, cols], x_scales[:, b, cols], True, True)
+
+        def height_centre(q):
+            if on_tensor(q):
+                t1_of[q] = padded[TENSOR_TILES.index(q % TILES)][:, :, D : D + ROW]
             else:
-                t1s[q] = t1_pool.tile([P, cw], F32, name="t1")
-            nc.scalar.activation(out=t1rows(q, 0, nh), in_=t0rows(q, h0, h0 + nh), func=COPY, scale=tap(0, 1, q % 8))
+                t1_of[q] = by_rows(t1_pool.tile([P, CHUNK], F32, name="t1")[:])
+            centre(t1_of[q], by_rows(own_bank[q][:]), 0, q % TILES)
 
-        def v_h(q):
-            b, h0, nh, cw = geo(q)
-            tl = q % 8
-            lo = 1 if h0 == 0 else 0
-            hi = nh - 1 if h0 + nh == H else nh
-            return [
-                lambda: stt(t1rows(q, lo, nh), t0rows(q, h0 + lo - 1, h0 + nh - 1), tap(0, 0, tl), t1rows(q, lo, nh)),
-                lambda: stt(t1rows(q, 0, hi), t0rows(q, h0 + 1, h0 + hi + 1), tap(0, 2, tl), t1rows(q, 0, hi)),
-            ]
+        def height_tap(q, k):
+            t1, own, shifted = t1_of[q], by_rows(own_bank[q][:]), by_rows(shifted_bank[q][:])
+            inside = CHUNK_ROWS - 1
+            if (first_row(q) == 0) == (k == 2):
+                add_tap(t1, shifted, 0, k, q % TILES)
+            elif k == 0:
+                add_tap(t1[:, 1:, :], own[:, 0:inside, :], 0, k, q % TILES)
+            else:
+                add_tap(t1[:, 0:inside, :], own[:, 1:, :], 0, k, q % TILES)
 
-        def s_wc(q):
-            t2s[q] = t2_pool.tile([P, geo(q)[3]], F32, name="t2")
-            nc.scalar.activation(out=t2s[q][:], in_=t1s[q][:], func=COPY, scale=tap(1, 1, q % 8))
-
-        def pe_w(q, taps):
-            nh, cw = geo(q)[2:4]
-            if 0 in taps:
-                bank = ps.tile([P, HALF], F32, name="bank")
-                t2s[q] = bank[:, 0:cw]
-            n_ = PE_TILES.index(q % 8)
-            for k in taps:
+        def width_on_tensor(q):
+            i = TENSOR_TILES.index(q % TILES)
+            t2_of[q] = banks.tile([P, CHUNK], F32, name="bank")
+            for k in range(3):
                 nc.tensor.matmul(
-                    out=rows(t2s[q][:], 0, nh),
-                    lhsT=diag[:, 3 * n_ + k, :],
-                    rhs=t1s[q][:, 0:nh, 16 * k : 16 * k + 128],
+                    out=by_rows(t2_of[q][:]),
+                    lhsT=diag[:, i, k, :],
+                    rhs=padded[i][:, :, k * D : k * D + ROW],
                     start=(k == 0),
                     stop=(k == 2),
                 )
 
-        def v_w(q):
-            tl, nh = q % 8, geo(q)[2]
-            a, o = rows(t1s[q][:], 0, nh), rows(t2s[q][:], 0, nh)
-            return [
-                lambda: stt(o[:, :, 16:128], a[:, :, 0:112], tap(1, 0, tl), o[:, :, 16:128]),
-                lambda: stt(o[:, :, 0:112], a[:, :, 16:128], tap(1, 2, tl), o[:, :, 0:112]),
-            ]
+        def width_centre(q):
+            t2_of[q] = t2_pool.tile([P, CHUNK], F32, name="t2")
+            centre(by_rows(t2_of[q][:]), t1_of[q], 1, q % TILES)
 
-        def s_dc(q):
-            key, cw = q // 4, geo(q)[3]
-            if key not in t3s:
-                t3s[key] = t3_pool.tile([P, 4, cw], F32, name="t3f")
-            nc.scalar.activation(out=t3s[key][:, q % 4, :], in_=t2s[q][:], func=COPY, scale=tap(2, 1, q % 8))
-
-        def v_d(q):
-            tl = q % 8
-            a = t2s[q][:].rearrange("p (r d) -> p r d", d=D)
-            o = t3s[q // 4][:, q % 4, :].rearrange("p (r d) -> p r d", d=D)
-            return [
-                lambda: stt(o[:, :, 1:16], a[:, :, 0:15], tap(2, 0, tl), o[:, :, 1:16]),
-                lambda: stt(o[:, :, 0:15], a[:, :, 1:16], tap(2, 2, tl), o[:, :, 0:15]),
-            ]
-
-        jobs = {}
-        grps, accs = {}, {}
-
-        def at(kind, step, fn):
-            jobs[(kind, step)] = jobs.get((kind, step), []) + [fn]
-
-        def run(kind, step):
-            for fn in jobs.get((kind, step), []):
-                fn()
-
-        def piece(copy, key, src, lo, hi):
-            if key not in grps:
-                grps[key] = new_grp()
-            regroup(copy, grps[key][:, lo:hi, :], src[:, :, lo:hi])
-
-        def uo_piece(g, hf, n_):
-            piece(scopy, ("uo", g, hf), uo_raw[:, g, :, hf * HALF : (hf + 1) * HALF], n_ * 256, (n_ + 1) * 256)
-
-        def uo_quant(g, hf):
-            cols = slice(hf * HALF, (hf + 1) * HALF)
-            quant(grps[("uo", g, hf)][:], uo_codes[:, g, cols], uo_scales[:, g, cols])
-
-        def t3_piece(copy, c, g, lo, hi):
-            piece(copy, ("t3", c, g), t3s[c * 2 + g][:], lo, hi)
-
-        def width(c):
-            return CHUNKS[c][2] * 128
-
-        def t3_quant(c, g):
-            cw = width(c)
-            quant(grps[("t3", c, g)][:, 0:cw, :], t3_codes[:, c, g, 0:cw], t3_scales[:, c, g, 0:cw])
-
-        def x1_regroup(hf):
-            grps[("x1", hf)] = new_grp()
-            regroup(scopy, grps[("x1", hf)][:], x_raw[:, 1, :, hf * HALF : (hf + 1) * HALF])
-
-        def x1_quant(hf):
-            cols = slice(hf * HALF, (hf + 1) * HALF)
-            quant(grps[("x1", hf)][:], x_codes[:, 1, cols], x_scales[:, 1, cols])
-
-        def pe_pass(c, k, g):
-            if g == 0:
-                accs[(c, k)] = ps.tile([P, HALF], F32, name="bank")
-            cc = slice(k * P, (k + 1) * P)
-            cw = width(c)
-            mx(accs[(c, k)][:, 0:cw], uo_codes[:, g, cc], uo_scales[:, g, cc], t3_codes[:, c, g, 0:cw], t3_scales[:, c, g, 0:cw], g == 0, g == 1)
-
-        def pe_group(c, k):
-            pe_pass(c, k, 0)
-            pe_pass(c, k, 1)
-
-        def evac(c, k, on_vector):
-            b, h0, nh = CHUNKS[c]
-            cw = width(c)
-            osb = o_pool.tile([P, cw], F32, name="osb")
-            if on_vector:
-                nc.vector.tensor_scalar(out=osb[:], in0=accs[(c, k)][:, 0:cw], scalar1=vecs[:, k, 9:10], scalar2=None, op0=ADD)
+        def width_tap(q, k):
+            t1, t2 = t1_of[q], by_rows(t2_of[q][:])
+            if k == 0:
+                add_tap(t2[:, :, D:ROW], t1[:, :, 0 : ROW - D], 1, k, q % TILES)
             else:
-                nc.scalar.activation(out=osb[:], in_=accs[(c, k)][:, 0:cw], func=IDENT, bias=vecs[:, k, 9:10], scale=1.0)
-            ov = out[b].rearrange("(i m) h w d -> i m (h w d)", m=P)
-            nc.sync.dma_start(out=ov[k][:, h0 * 128 : h0 * 128 + cw], in_=osb[:])
+                add_tap(t2[:, :, 0 : ROW - D], t1[:, :, D:ROW], 1, k, q % TILES)
 
-        at("V", 0, lambda: quant(g_ui1[:], ui_codes[:, HALF:R], ui_scales[:, HALF:R]))
-        for n_, (g, hf, st) in enumerate(((0, 0, 4), (1, 0, 6), (0, 1, 10), (1, 1, 14))):
-            at("S", st, lambda g=g, hf=hf: uo_piece(g, hf, 0))
-            at("S", st + 1, lambda g=g, hf=hf: uo_piece(g, hf, 1))
-            at("V", st + 2, lambda g=g, hf=hf: uo_quant(g, hf))
-        for hf in range(2):
-            at("S", 9 + 2 * hf, lambda hf=hf: x1_regroup(hf))
-            at("V", 10 + 2 * hf, lambda hf=hf: x1_quant(hf))
-        for c in range(NC):
-            for g in range(2):
-                if (c, g) != (NC - 1, 1):
-                    st = 8 * c + 4 * g + 8
-                    at("S", st, lambda c=c, g=g: t3_piece(scopy, c, g, 0, 256))
-                    if width(c) > 256:
-                        at("S", st + 1, lambda c=c, g=g: t3_piece(scopy, c, g, 256, 512))
-                    at("V", st + 2, lambda c=c, g=g: t3_quant(c, g))
-        for c in range(NC - 1):
-            for k in range(8):
-                st = 8 * c + 15 + (k if c < NC - 2 else k // 2)
-                at("PE", st, lambda c=c, k=k: pe_group(c, k))
-                at("E", st + 1, lambda c=c, k=k: evac(c, k, False))
+        def t3_plane(q):
+            return by_depth(t3_of[q // PASS_TILES][:, q % PASS_TILES, :])
 
-        for s in range(-1, NU + 4):
-            if valid(s + 1):
-                pe_t0(s + 1)
-            run("PE", s)
-            if valid(s - 2) and on_pe(s - 2):
-                pe_w(s - 2, (1, 2))
-            if valid(s - 1) and on_pe(s - 1):
-                pe_w(s - 1, (0,))
-            run("E", s)
-            if valid(s - 1) and not on_pe(s - 1):
-                s_wc(s - 1)
-            if valid(s - 4) and on_pe(s - 4):
-                s_dc(s - 4)
-            if valid(s - 3) and not on_pe(s - 3):
-                s_dc(s - 3)
-            if valid(s + 1):
-                s_hc(s + 1)
-            ops = [
-                v_h(s) if valid(s) else [],
-                v_w(s - 2) if valid(s - 2) and not on_pe(s - 2) else [],
-                v_d(s - 5) if valid(s - 5) and on_pe(s - 5) else [],
-                v_d(s - 4) if valid(s - 4) and not on_pe(s - 4) else [],
-            ]
-            for n_ in range(2):
-                for lst in ops:
-                    if lst:
-                        lst[n_]()
-            run("V", s)
-            run("S", s)
+        def depth_centre(q):
+            if q % PASS_TILES == 0:
+                t3_of[q // PASS_TILES] = t3_pool.tile([P, PASS_TILES, CHUNK], F32, name="t3")
+            centre(t3_plane(q), by_depth(t2_of[q][:]), 2, q % TILES)
 
-        last = NC - 1
-        for k in range(8):
-            pe_pass(last, k, 0)
-        t3_piece(scopy, last, 1, 0, width(last) // 2)
-        t3_piece(vcopy, last, 1, width(last) // 2, width(last))
-        t3_quant(last, 1)
-        for k in range(8):
-            pe_pass(last, k, 1)
-            evac(last, k, k % 2 == 1)
+        def depth_tap(q, k):
+            t2, t3 = by_depth(t2_of[q][:]), t3_plane(q)
+            if k == 0:
+                add_tap(t3[:, :, 1:D], t2[:, :, 0 : D - 1], 2, k, q % TILES)
+            else:
+                add_tap(t3[:, :, 0 : D - 1], t2[:, :, 1:D], 2, k, q % TILES)
+
+        def regroup_t3(copy, p, half):
+            if half == 0:
+                grouped_of[p] = new_grouped()
+            cols = slice(half * 256, (half + 1) * 256)
+            regroup(copy, grouped_of[p][:, cols, :], t3_of[p][:, :, cols])
+
+        def quantise_t3(p):
+            quantise(grouped_of[p][:], t3_codes[:, p // 2, p % 2, :], t3_scales[:, p // 2, p % 2, :])
+
+        def second_matmul(c, k, g):
+            if g == 0:
+                acc_of[(c, k)] = banks.tile([P, CHUNK], F32, name="bank")
+            w_cols = slice(k * P, (k + 1) * P)
+            mx(acc_of[(c, k)][:], uo_codes[:, g, w_cols], uo_scales[:, g, w_cols], t3_codes[:, c, g, :], t3_scales[:, c, g, :], g == 0, g == 1)
+
+        def store(c, k, engine):
+            result = out_pool.tile([P, CHUNK], F32, name="result")
+            if engine == "vector":
+                nc.vector.tensor_scalar(out=result[:], in0=acc_of[(c, k)][:], scalar1=vecs[:, k, 9:10], scalar2=None, op0=ADD)
+            else:
+                nc.scalar.activation(out=result[:], in_=acc_of[(c, k)][:], func=IDENTITY, bias=vecs[:, k, 9:10], scale=1.0)
+            col = (c * CHUNK) % N
+            out_view = out[c * CHUNK // N].rearrange("(i m) h w d -> i m (h w d)", m=P)
+            nc.sync.dma_start(out=out_view[k][:, col : col + CHUNK], in_=result[:])
+
+        def regroup_uo(quarter, half):
+            g, col = quarter % 2, quarter // 2 * 512 + half * 256
+            if half == 0:
+                grouped_of[("uo", quarter)] = new_grouped()
+            regroup(on_scalar, grouped_of[("uo", quarter)][:, half * 256 : (half + 1) * 256, :], uo_raw[:, g, :, col : col + 256])
+
+        def quantise_uo(quarter):
+            g, cols = quarter % 2, slice(quarter // 2 * 512, (quarter // 2 + 1) * 512)
+            quantise(grouped_of[("uo", quarter)][:], uo_codes[:, g, cols], uo_scales[:, g, cols])
+
+        for s in range(-1, UNITS + TILES + 1):
+            if is_unit(s + 1):
+                first_matmul(s + 1)
+            c, k = divmod(s - 15, TILES)
+            if 0 <= c < CHUNKS - 1:
+                second_matmul(c, k, 0)
+                second_matmul(c, k, 1)
+            if is_unit(s - 1) and on_tensor(s - 1):
+                width_on_tensor(s - 1)
+            c, k = divmod(s - 16, TILES)
+            if 0 <= c < CHUNKS - 1:
+                store(c, k, "scalar")
+            if is_unit(s - 1) and not on_tensor(s - 1):
+                width_centre(s - 1)
+            if is_unit(s - 3):
+                depth_centre(s - 3)
+            if is_unit(s + 1):
+                height_centre(s + 1)
+            for k in (0, 2):
+                if is_unit(s):
+                    height_tap(s, k)
+                if is_unit(s - 2) and not on_tensor(s - 2):
+                    width_tap(s - 2, k)
+                if is_unit(s - 4):
+                    depth_tap(s - 4, k)
+            if s in (1, 2):
+                quantise_ui(ui_hi, 256 + s * 256, 512 + s * 256)
+            p, i = divmod(s - 4, 4)
+            if 0 <= p < 4 and i == 0:
+                quantise_uo(p)
+            if s in (10, 12):
+                quantise_x(x1_grouped, 1, (s - 10) // 2)
+            p, i = divmod(s - 10, PASS_TILES)
+            if 0 <= p < PASSES - 1 and i == 0:
+                quantise_t3(p)
+            if s in (0, 1):
+                prepare_ui(on_scalar, ui_hi, 512 + s * 256, 768 + s * 256)
+            p, i = divmod(s - 2, 4)
+            if 0 <= p < 4 and i < 2:
+                regroup_uo(p, i)
+            if s in (9, 11):
+                x1_grouped = prepare_x(on_scalar, 1, (s - 9) // 2)
+            p, i = divmod(s - 8, PASS_TILES)
+            if 0 <= p < PASSES - 1 and i < 2:
+                regroup_t3(on_scalar, p, i)
+
+        c = CHUNKS - 1
+        for k in range(CO // P):
+            second_matmul(c, k, 0)
+        regroup_t3(on_scalar, PASSES - 1, 0)
+        regroup_t3(on_vector, PASSES - 1, 1)
+        quantise_t3(PASSES - 1)
+        for k in range(CO // P):
+            second_matmul(c, k, 1)
+            store(c, k, "vector" if k % 2 == 1 else "scalar")

@@ -24,7 +24,7 @@ CHUNKS = B * N // CHUNK
 TILES = R // P
 PASS_TILES = PACK
 PADDED_ROW = ROW + 2 * D
-TENSOR_TILES = (1, 4, 6)
+TENSOR_TILES = ()
 UNITS = CHUNKS * TILES
 PASSES = 2 * CHUNKS
 FLOPS = 2 * B * N * (CI * R + R * CO) + 2 * 9 * B * R * N
@@ -70,7 +70,7 @@ def tile_lowrankconv3d_pa_kernel(tc, x, U_k_h, U_k_w, U_k_d, U_c_in, U_c_out, bi
         vec_rows = keep.tile([P, R], BF16, name="vec_rows")
         vecs = keep.tile([P, TILES, 10], F32, name="vecs")
         ident = keep.tile([P, P], BF16, name="ident")
-        diag = keep.tile([P, len(TENSOR_TILES), 3, P], F32, name="diag")
+        diag = None
         padded = [keep.tile([P, CHUNK_ROWS, PADDED_ROW], F32, name="padded%d" % i) for i in range(len(TENSOR_TILES))]
 
         nc.vector.memset(vec_rows[:], 0.0)

from contextlib import ExitStack

import concourse.mybir as mybir
from concourse.masks import make_identity

F32 = mybir.dt.float32
BF16 = mybir.dt.bfloat16
U32 = mybir.dt.uint32
U8 = mybir.dt.uint8
FP8X4 = mybir.dt.float8_e4m3fn_x4
MULT = mybir.AluOpType.mult
ADD = mybir.AluOpType.add
COPY = mybir.ActivationFunctionType.Copy
IDENTITY = mybir.ActivationFunctionType.Identity

P = 128
PACK = 4
B, CI, R, CO, H, W, D = 2, 512, 1024, 1024, 8, 8, 16
N = H * W * D
ROW = W * D
CHUNK_ROWS = 4
CHUNK = CHUNK_ROWS * ROW
CHUNKS = B * N // CHUNK
TILES = R // P
PASS_TILES = PACK
PADDED_ROW = ROW + 2 * D
TENSOR_TILES = ()
UNITS = CHUNKS * TILES
PASSES = 2 * CHUNKS
FLOPS = 2 * B * N * (CI * R + R * CO) + 2 * 9 * B * R * N


def regroup(copy, dst, src):
    copy(
        out=dst.rearrange("p (c i) t -> p c t i", i=4),
        in_=src.rearrange("p t (c i) -> p c t i", i=4),
    )


def by_rows(ap):
    return ap.rearrange("p (h c) -> p h c", c=ROW)


def by_depth(ap):
    return ap.rearrange("p (r d) -> p r d", d=D)


def tile_lowrankconv3d_pa_kernel(tc, x, U_k_h, U_k_w, U_k_d, U_c_in, U_c_out, bias, out):
    nc = tc.nc
    with ExitStack() as ctx:
        keep = ctx.enter_context(tc.tile_pool(name="keep", bufs=1))
        grouped_pool = ctx.enter_context(tc.tile_pool(name="grouped", bufs=4))
        t1_pool = ctx.enter_context(tc.tile_pool(name="t1", bufs=6))
        t2_pool = ctx.enter_context(tc.tile_pool(name="t2", bufs=6))
        t3_pool = ctx.enter_context(tc.tile_pool(name="t3", bufs=3))
        out_pool = ctx.enter_context(tc.tile_pool(name="out", bufs=8))
        banks = ctx.enter_context(tc.psum_pool(name="banks", bufs=8))

        x_raw = keep.tile([P, B, PACK, N], BF16, name="x_raw")
        ui_raw = keep.tile([P, PACK, R], BF16, name="ui_raw")
        uo_raw = keep.tile([P, 2, PACK, CO], BF16, name="uo_raw")
        x_codes = keep.tile([P, B, N], U32, name="x_codes", align_bytes=64)
        x_scales = keep.tile([P, B, N], U8, name="x_scales", align_bytes=64)
        ui_codes = keep.tile([P, R], U32, name="ui_codes", align_bytes=64)
        ui_scales = keep.tile([P, R], U8, name="ui_scales", align_bytes=64)
        uo_codes = keep.tile([P, 2, CO], U32, name="uo_codes", align_bytes=64)
        uo_scales = keep.tile([P, 2, CO], U8, name="uo_scales", align_bytes=64)
        t3_codes = keep.tile([P, CHUNKS, 2, CHUNK], U32, name="t3_codes", align_bytes=64)
        t3_scales = keep.tile([P, CHUNKS, 2, CHUNK], U8, name="t3_scales", align_bytes=64)
        vec_rows = keep.tile([P, R], BF16, name="vec_rows")
        vecs = keep.tile([P, TILES, 10], F32, name="vecs")
        ident = keep.tile([P, P], BF16, name="ident")
        diag = None
        padded = [keep.tile([P, CHUNK_ROWS, PADDED_ROW], F32, name="padded%d" % i) for i in range(len(TENSOR_TILES))]

        nc.vector.memset(vec_rows[:], 0.0)
        make_identity(nc, ident[:])
        for t in padded:
            nc.vector.memset(t[:], 0.0)

        for f, u in enumerate((U_k_h, U_k_w, U_k_d)):
            nc.scalar.dma_start(out=vec_rows[3 * f : 3 * f + 3, :], in_=u)
        nc.scalar.dma_start(out=vec_rows[9:10, :], in_=bias.rearrange("(o c) -> o c", o=1))
        x_view = [x[b].rearrange("(p t) h w d -> p t (h w d)", t=PACK) for b in range(B)]
        ui_view = U_c_in.rearrange("(p t) r -> p t r", t=PACK)
        uo_view = U_c_out.rearrange("(g t p) c -> g p t c", g=2, t=PACK)
        nc.sync.dma_start(out=ui_raw[:, :, 0:P], in_=ui_view[:, :, 0:P])
        nc.sync.dma_start(out=x_raw[:, 0, :, 0:CHUNK], in_=x_view[0][:, :, 0:CHUNK])
        nc.sync.dma_start(out=x_raw[:, 0, :, CHUNK:N], in_=x_view[0][:, :, CHUNK:N])
        nc.sync.dma_start(out=ui_raw[:, :, P:512], in_=ui_view[:, :, P:512])
        nc.sync.dma_start(out=ui_raw[:, :, 512:R], in_=ui_view[:, :, 512:R])
        nc.sync.dma_start(out=uo_raw[:, 0, :, :], in_=uo_view[0])
        nc.sync.dma_start(out=uo_raw[:, 1, :, :], in_=uo_view[1])
        nc.sync.dma_start(out=x_raw[:, 1, :, :], in_=x_view[1])

        on_vector = nc.vector.tensor_copy
        on_scalar = nc.scalar.copy

        def new_grouped():
            return grouped_pool.tile([P, 512, PACK], BF16, name="grouped", align_bytes=64)

        def quantise(grouped, codes, scales):
            nc.vector.quantize_mx(out=codes.bitcast(FP8X4), scales=scales, in_=grouped.rearrange("p w t -> p (w t)"))

        def mx(acc, w_codes, w_scales, m_codes, m_scales, start, stop):
            nc.tensor.matmul_mx(
                out=acc,
                lhsT=w_codes.bitcast(FP8X4),
                lhsT_scale=w_scales,
                rhs=m_codes.bitcast(FP8X4),
                rhs_scale=m_scales,
                start=start,
                stop=stop,
            )

        def tap(axis, k, tl):
            return vecs[:, tl, 3 * axis + k : 3 * axis + k + 1]

        def centre(dst, src, axis, tl):
            nc.scalar.activation(out=dst, in_=src, func=COPY, scale=tap(axis, 1, tl))

        def add_tap(acc, src, axis, k, tl):
            nc.vector.scalar_tensor_tensor(out=acc, in0=src, scalar=tap(axis, k, tl), in1=acc, op0=MULT, op1=ADD)

        vec_bank = banks.tile([P, TILES, P], BF16, name="bank")
        for i in range(TILES):
            nc.tensor.transpose(vec_bank[:, i, :], vec_rows[:, i * P : (i + 1) * P], ident[:])
        nc.scalar.copy(out=vecs[:], in_=vec_bank[:, :, 0:10])
        for i, tl in enumerate(TENSOR_TILES):
            for k in range(3):
                nc.scalar.activation(out=diag[:, i, k, :], in_=ident[:], func=COPY, scale=tap(1, k, tl))

        def prepare_ui(copy, grouped, lo, hi):
            regroup(copy, grouped[:, lo % 512 : (hi - 1) % 512 + 1, :], ui_raw[:, :, lo:hi])

        def quantise_ui(grouped, lo, hi):
            quantise(grouped[:, lo % 512 : (hi - 1) % 512 + 1, :], ui_codes[:, lo:hi], ui_scales[:, lo:hi])

        def prepare_x(copy, b, half):
            cols = slice(half * 512, (half + 1) * 512)
            grouped = new_grouped()
            regroup(copy, grouped[:], x_raw[:, b, :, cols])
            return grouped

        def quantise_x(grouped, b, half):
            cols = slice(half * 512, (half + 1) * 512)
            quantise(grouped[:], x_codes[:, b, cols], x_scales[:, b, cols])

        ui_lo = new_grouped()
        prepare_ui(on_vector, ui_lo, 0, P)
        x00 = prepare_x(on_vector, 0, 0)
        quantise_ui(ui_lo, 0, P)
        quantise_x(x00, 0, 0)
        x01 = prepare_x(on_vector, 0, 1)
        prepare_ui(on_scalar, ui_lo, P, 512)
        quantise_x(x01, 0, 1)
        quantise_ui(ui_lo, P, 2 * P)
        quantise_ui(ui_lo, 2 * P, 512)
        ui_hi = new_grouped()


        own_bank, shifted_bank, t1_of, t2_of, t3_of, grouped_of, acc_of = {}, {}, {}, {}, {}, {}, {}

        def is_unit(q):
            return 0 <= q < UNITS

        def on_tensor(q):
            return q % TILES in TENSOR_TILES

        def first_row(q):
            return (q // TILES * CHUNK_ROWS) % H

        def first_matmul(q):
            b, h0, tl = q // TILES * CHUNK // N, first_row(q), q % TILES
            w_cols = slice(tl * P, (tl + 1) * P)
            own_bank[q] = banks.tile([P, CHUNK], F32, name="bank")
            shifted_bank[q] = banks.tile([P, CHUNK], F32, name="bank")
            for bank, row in ((own_bank[q], h0), (shifted_bank[q], h0 + 1 if h0 == 0 else h0 - 1)):
                cols = slice(row * ROW, row * ROW + CHUNK)
                mx(bank[:], ui_codes[:, w_cols], ui_scales[:, w_cols], x_codes[:, b, cols], x_scales[:, b, cols], True, True)

        def height_centre(q):
            if on_tensor(q):
                t1_of[q] = padded[TENSOR_TILES.index(q % TILES)][:, :, D : D + ROW]
            else:
                t1_of[q] = by_rows(t1_pool.tile([P, CHUNK], F32, name="t1")[:])
            centre(t1_of[q], by_rows(own_bank[q][:]), 0, q % TILES)

        def height_tap(q, k):
            t1, own, shifted = t1_of[q], by_rows(own_bank[q][:]), by_rows(shifted_bank[q][:])
            inside = CHUNK_ROWS - 1
            if (first_row(q) == 0) == (k == 2):
                add_tap(t1, shifted, 0, k, q % TILES)
            elif k == 0:
                add_tap(t1[:, 1:, :], own[:, 0:inside, :], 0, k, q % TILES)
            else:
                add_tap(t1[:, 0:inside, :], own[:, 1:, :], 0, k, q % TILES)

        def width_on_tensor(q):
            i = TENSOR_TILES.index(q % TILES)
            t2_of[q] = banks.tile([P, CHUNK], F32, name="bank")
            for k in range(3):
                nc.tensor.matmul(
                    out=by_rows(t2_of[q][:]),
                    lhsT=diag[:, i, k, :],
                    rhs=padded[i][:, :, k * D : k * D + ROW],
                    start=(k == 0),
                    stop=(k == 2),
                )

        def width_centre(q):
            t2_of[q] = t2_pool.tile([P, CHUNK], F32, name="t2")
            centre(by_rows(t2_of[q][:]), t1_of[q], 1, q % TILES)

        def width_tap(q, k):
            t1, t2 = t1_of[q], by_rows(t2_of[q][:])
            if k == 0:
                add_tap(t2[:, :, D:ROW], t1[:, :, 0 : ROW - D], 1, k, q % TILES)
            else:
                add_tap(t2[:, :, 0 : ROW - D], t1[:, :, D:ROW], 1, k, q % TILES)

        def t3_plane(q):
            return by_depth(t3_of[q // PASS_TILES][:, q % PASS_TILES, :])

        def depth_centre(q):
            if q % PASS_TILES == 0:
                t3_of[q // PASS_TILES] = t3_pool.tile([P, PASS_TILES, CHUNK], F32, name="t3")
            centre(t3_plane(q), by_depth(t2_of[q][:]), 2, q % TILES)

        def depth_tap(q, k):
            t2, t3 = by_depth(t2_of[q][:]), t3_plane(q)
            if k == 0:
                add_tap(t3[:, :, 1:D], t2[:, :, 0 : D - 1], 2, k, q % TILES)
            else:
                add_tap(t3[:, :, 0 : D - 1], t2[:, :, 1:D], 2, k, q % TILES)

        def regroup_t3(copy, p, half):
            if half == 0:
                grouped_of[p] = new_grouped()
            cols = slice(half * 256, (half + 1) * 256)
            regroup(copy, grouped_of[p][:, cols, :], t3_of[p][:, :, cols])

        def quantise_t3(p):
            quantise(grouped_of[p][:], t3_codes[:, p // 2, p % 2, :], t3_scales[:, p // 2, p % 2, :])

        def second_matmul(c, k, g):
            if g == 0:
                acc_of[(c, k)] = banks.tile([P, CHUNK], F32, name="bank")
            w_cols = slice(k * P, (k + 1) * P)
            mx(acc_of[(c, k)][:], uo_codes[:, g, w_cols], uo_scales[:, g, w_cols], t3_codes[:, c, g, :], t3_scales[:, c, g, :], g == 0, g == 1)

        def store(c, k, engine):
            result = out_pool.tile([P, CHUNK], F32, name="result")
            if engine == "vector":
                nc.vector.tensor_scalar(out=result[:], in0=acc_of[(c, k)][:], scalar1=vecs[:, k, 9:10], scalar2=None, op0=ADD)
            else:
                nc.scalar.activation(out=result[:], in_=acc_of[(c, k)][:], func=IDENTITY, bias=vecs[:, k, 9:10], scale=1.0)
            col = (c * CHUNK) % N
            out_view = out[c * CHUNK // N].rearrange("(i m) h w d -> i m (h w d)", m=P)
            nc.sync.dma_start(out=out_view[k][:, col : col + CHUNK], in_=result[:])

        def regroup_uo(quarter, half):
            g, col = quarter % 2, quarter // 2 * 512 + half * 256
            if half == 0:
                grouped_of[("uo", quarter)] = new_grouped()
            regroup(on_scalar, grouped_of[("uo", quarter)][:, half * 256 : (half + 1) * 256, :], uo_raw[:, g, :, col : col + 256])

        def quantise_uo(quarter):
            g, cols = quarter % 2, slice(quarter // 2 * 512, (quarter // 2 + 1) * 512)
            quantise(grouped_of[("uo", quarter)][:], uo_codes[:, g, cols], uo_scales[:, g, cols])

        for s in range(-1, UNITS + TILES + 1):
            if is_unit(s + 1):
                first_matmul(s + 1)
            c, k = divmod(s - 15, TILES)
            if 0 <= c < CHUNKS - 1:
                second_matmul(c, k, 0)
                second_matmul(c, k, 1)
            if is_unit(s - 1) and on_tensor(s - 1):
                width_on_tensor(s - 1)
            c, k = divmod(s - 16, TILES)
            if 0 <= c < CHUNKS - 1:
                store(c, k, "scalar")
            if is_unit(s - 1) and not on_tensor(s - 1):
                width_centre(s - 1)
            if is_unit(s - 3):
                depth_centre(s - 3)
            if is_unit(s + 1):
                height_centre(s + 1)
            for k in (0, 2):
                if is_unit(s):
                    height_tap(s, k)
                if is_unit(s - 2) and not on_tensor(s - 2):
                    width_tap(s - 2, k)
                if is_unit(s - 4):
                    depth_tap(s - 4, k)
            if s in (1, 2):
                quantise_ui(ui_hi, 256 + s * 256, 512 + s * 256)
            p, i = divmod(s - 4, 4)
            if 0 <= p < 4 and i == 0:
                quantise_uo(p)
            if s in (10, 12):
                quantise_x(x1_grouped, 1, (s - 10) // 2)
            p, i = divmod(s - 10, PASS_TILES)
            if 0 <= p < PASSES - 1 and i == 0:
                quantise_t3(p)
            if s in (0, 1):
                prepare_ui(on_scalar, ui_hi, 512 + s * 256, 768 + s * 256)
            p, i = divmod(s - 2, 4)
            if 0 <= p < 4 and i < 2:
                regroup_uo(p, i)
            if s in (9, 11):
                x1_grouped = prepare_x(on_scalar, 1, (s - 9) // 2)
            p, i = divmod(s - 8, PASS_TILES)
            if 0 <= p < PASSES - 1 and i < 2:
                regroup_t3(on_scalar, p, i)

        c = CHUNKS - 1
        for k in range(CO // P):
            second_matmul(c, k, 0)
        regroup_t3(on_scalar, PASSES - 1, 0)
        regroup_t3(on_vector, PASSES - 1, 1)
        quantise_t3(PASSES - 1)
        for k in range(CO // P):
            second_matmul(c, k, 1)
            store(c, k, "vector" if k % 2 == 1 else "scalar")
